import numpy as np
import ml_dtypes


def mxq(x, axis, fmt="e4m3"):
    dtype, down = {"e4m3": (ml_dtypes.float8_e4m3fn, 7), "e5m2": (ml_dtypes.float8_e5m2, 14)}[fmt]
    v = np.moveaxis(np.asarray(x, np.float32).astype(ml_dtypes.bfloat16).astype(np.float64), axis, -1)
    blocks = v.reshape(v.shape[:-1] + (-1, 32))
    amax = np.abs(blocks).max(-1, keepdims=True)
    byte = np.maximum(np.where(amax > 0, np.frexp(amax)[1] - 1 + 127, 0) - down, 1)
    scale = np.exp2(byte - 127.0)
    codes = (blocks / scale).astype(np.float32).astype(dtype).astype(np.float64)
    return np.moveaxis((codes * scale).reshape(v.shape), -1, axis)


WIDE = False


def mx_kscale(k):
    if not WIDE:
        return np.ones(k)
    levels = np.array([10, -10, 5, -5, 0])
    if k % 512:
        return np.exp2(np.random.permutation(np.resize(levels, k // 32))).repeat(32)
    a = np.empty((k // 512, 16))
    for p in range(k // 512):
        a[p, :8] = np.random.permutation(np.resize(levels, 8))
        for g in range(8):
            far = levels[np.abs(levels - a[p, g]) >= 10]
            a[p, g + 8] = far[np.random.randint(len(far))]
    return np.exp2(a.ravel()).repeat(32)


BF16 = ml_dtypes.bfloat16


def bf(x):
    return np.asarray(x, np.float32).astype(BF16)


def f64(x):
    return np.asarray(x).astype(np.float64)


E2M1 = np.array([0.0, 0.5, 1.0, 1.5, 2.0, 3.0, 4.0, 6.0, -0.0, -0.5, -1.0, -1.5, -2.0, -3.0, -4.0, -6.0])


def pack_weight(w, fmt):
    k, n = w.shape
    w = f64(bf(w)).reshape(k // 32, 32, n)
    amax = np.abs(w).max(1)
    if fmt == "e4m3":
        byte = np.frexp(amax)[1] - 1 + 127 - 7
    else:
        mant, ex = np.frexp(amax / 6.0)
        byte = np.where(mant > 0.5, ex, ex - 1) + 127
    byte = np.clip(np.where(amax > 0, byte, 1), 1, 254)
    scaled = (w * np.exp2(127.0 - byte)[:, None, :]).reshape(k, n).astype(np.float32)
    by_word = np.ascontiguousarray(scaled.reshape(k // 512, 128, 4, n).transpose(0, 1, 3, 2))
    if fmt == "e4m3":
        words = by_word.astype(ml_dtypes.float8_e4m3fn).view(np.uint8)
    else:
        c = by_word.astype(ml_dtypes.float4_e2m1fn).view(np.uint8) & 0xF
        words = c[..., 0::2] | (c[..., 1::2] << 4)
    return np.ascontiguousarray(words), np.ascontiguousarray(byte.astype(np.uint8).reshape(k // 512, 16, n))


def unpack_weight(words, scales, fmt):
    g, p, n, _ = words.shape
    if fmt == "e4m3":
        vals = np.ascontiguousarray(words).view(ml_dtypes.float8_e4m3fn).astype(np.float64)
    else:
        nib = np.empty((g, p, n, 4), np.uint8)
        nib[..., 0::2] = words & 0xF
        nib[..., 1::2] = words >> 4
        vals = E2M1[nib]
    vals = vals * np.repeat(np.exp2(scales.astype(np.float64) - 127.0), 8, axis=1)[..., None]
    return vals.transpose(0, 1, 3, 2).reshape(g * 512, n)


B, F, H1, E, N, P, L, C, S = 2048, 2048, 512, 512, 32, 8, 100, 16, 100
EPS = 1e-5


def layernorm(x, g, b):
    mu = x.mean(axis=-1, keepdims=True)
    var = x.var(axis=-1, keepdims=True)
    return (x - mu) / np.sqrt(var + EPS) * g + b


def setup_inputs():
    rn = np.random.standard_normal
    s = mx_kscale(H1)
    t = mx_kscale(E)
    h1 = bf(np.maximum(rn((B, H1)), 0.0) * s)
    W2_words, W2_scales = pack_weight(rn((H1, E)) / np.sqrt(H1) / s[:, None], "e4m3")
    return {"h1": h1,
            "W2_words": W2_words,
            "W2_scales": W2_scales,
            "b2": bf(rn(E) * 0.3),
            "ln_g": bf((1.0 + 0.2 * rn(E)) * t),
            "ln_b": bf(0.3 * rn(E) * t),
            "pc_W": bf(rn((N, E, P)) / np.sqrt(E) / t[None, :, None]),
            "pc_b": bf(0.3 * rn((N, P))),
            "pc_g": bf(1.0 + 0.2 * rn((N, P))),
            "pc_beta": bf(0.3 * rn((N, P)))}


def reference(h1, W2_words, W2_scales, b2, ln_g, ln_b, pc_W, pc_b, pc_g, pc_beta):
    z = np.maximum((mxq(f64(h1), 1, "e4m3") @ unpack_weight(W2_words, W2_scales, "e4m3")) + f64(b2), 0.0)
    h = layernorm(z, f64(ln_g), f64(ln_b))
    w = mxq(f64(pc_W), 1, "e4m3").transpose(1, 0, 2).reshape(E, N * P)
    prim = (mxq(h, 1, "e4m3") @ w).reshape(B, N, P) + f64(pc_b)[None]
    return layernorm(prim, f64(pc_g)[None], f64(pc_beta)[None])

@@ -1,0 +1,258 @@
+from contextlib import ExitStack
+
+import concourse.mybir as mybir
+from concourse.masks import make_identity
+
+F32 = mybir.dt.float32
+BF16 = mybir.dt.bfloat16
+I32 = mybir.dt.int32
+U32 = mybir.dt.uint32
+U8 = mybir.dt.uint8
+FP8X4 = mybir.dt.float8_e4m3fn_x4
+ALU = mybir.AluOpType
+ACT = mybir.ActivationFunctionType
+AXIS = mybir.AxisListType
+
+P = 128
+PACK = 4
+B, H1, E = 2048, 512, 512
+CAPS, CAP_DIM = 32, 8
+NP = CAPS * CAP_DIM
+NP_TILES = NP // P
+TILES = B // P
+EPS = 1e-5
+
+FLOPS = 2 * B * H1 * E + 2 * B * E * NP
+
+
+def tile_hotpatchcapsmodel_pa_kernel(
+    tc, h1, W2_words, W2_scales, b2, ln_g, ln_b, pc_W, pc_b, pc_g, pc_beta, out
+):
+    nc = tc.nc
+    with ExitStack() as ctx:
+        keep = ctx.enter_context(tc.tile_pool(name="keep", bufs=1))
+        work = ctx.enter_context(tc.tile_pool(name="work", bufs=4))
+        psum = ctx.enter_context(tc.psum_pool(name="psum", bufs=1))
+
+        h1_rows = h1.rearrange("(p t) k -> p t k", t=TILES)
+        out_rows = out.rearrange("(p t) n q -> p t (n q)", t=TILES)
+
+        w2_plane = keep.tile([P, E], U8, align_bytes=64)
+        nc.vector.memset(w2_plane[:].bitcast(I32), 0)
+        b2_rows = keep.tile([P, P], BF16)
+        nc.vector.memset(b2_rows[:], 0.0)
+        other_rows = keep.tile([P, P], BF16)
+        nc.vector.memset(other_rows[:], 0.0)
+        eps = keep.tile([P, 1], F32)
+        nc.vector.memset(eps[:], EPS)
+
+        h1_sb = keep.tile([P, TILES, H1], BF16)
+        nc.sync.dma_start(out=h1_sb[:, 0:2, :], in_=h1_rows[:, 0:2, :])
+        w2_codes = keep.tile([P, E], U32, align_bytes=64)
+        nc.sync.dma_start(
+            out=w2_codes[:].bitcast(I32),
+            in_=W2_words[0].rearrange("p n t -> p (n t)").bitcast(I32),
+        )
+        for quadrant in range(4):
+            nc.sync.dma_start(
+                out=w2_plane[32 * quadrant : 32 * quadrant + 4, :].bitcast(I32),
+                in_=W2_scales[0, 4 * quadrant : 4 * quadrant + 4, :].bitcast(I32),
+            )
+        nc.sync.dma_start(out=b2_rows[0:4, :], in_=b2.rearrange("(j c) -> j c", c=P))
+        nc.sync.dma_start(out=other_rows[0:2, :], in_=pc_g.rearrange("(c n) q -> c (n q)", c=NP_TILES))
+        nc.sync.dma_start(out=other_rows[2:4, :], in_=pc_beta.rearrange("(c n) q -> c (n q)", c=NP_TILES))
+        nc.sync.dma_start(out=other_rows[4:6, :], in_=pc_b.rearrange("(c n) q -> c (n q)", c=NP_TILES))
+        ln_g_raw = keep.tile([P, PACK], BF16)
+        nc.sync.dma_start(out=ln_g_raw[:], in_=ln_g.rearrange("(p j) -> p j", j=PACK))
+        ln_b_raw = keep.tile([P, PACK], BF16)
+        nc.sync.dma_start(out=ln_b_raw[:], in_=ln_b.rearrange("(p j) -> p j", j=PACK))
+        pw_sb = keep.tile([P, CAPS, PACK * CAP_DIM], BF16)
+        nc.sync.dma_start(out=pw_sb[:], in_=pc_W.rearrange("n (p j) q -> p n (j q)", j=PACK))
+        for doubling in range(1, 4):
+            first = 2**doubling
+            nc.sync.dma_start(out=h1_sb[:, first : 2 * first, :], in_=h1_rows[:, first : 2 * first, :])
+
+        warm = keep.tile([P, 1], F32)
+        nc.scalar.activation(out=warm[:], in_=eps[:], func=ACT.Abs_reciprocal_sqrt)
+
+        ident_f = keep.tile([P, P], F32)
+        make_identity(nc, ident_f[:])
+        ident_b = keep.tile([P, P], BF16)
+        make_identity(nc, ident_b[:])
+
+        def to_columns(rows, count, tag):
+            rows_t = psum.tile([P, P], BF16, name="rows_t", tag=tag, bufs=2)
+            nc.tensor.transpose(rows_t[:], rows[:], ident_b[:])
+            columns = keep.tile([P, count], F32, name="columns_" + tag)
+            nc.vector.tensor_copy(out=columns[:], in_=rows_t[:, 0:count])
+            return columns
+
+        def along_free_axis(columns, tag):
+            repeated = keep.tile([P, 4, P], F32, name="repeated_" + tag)
+            nc.vector.tensor_copy(out=repeated[:], in_=columns.unsqueeze(2).to_broadcast([P, 4, P]))
+            spread = psum.tile([P, 4, P], F32, name="spread", tag=tag, bufs=2)
+            for k in range(4):
+                nc.tensor.transpose(spread[:, k, :], repeated[:, k, :], ident_f[:])
+            everywhere = keep.tile([P, 4 * P], F32, name="everywhere_" + tag)
+            nc.vector.tensor_copy(out=everywhere[:], in_=spread[:].rearrange("p k c -> p (k c)"))
+            return everywhere
+
+        b2_bc = along_free_axis(to_columns(b2_rows, 4, "normed_t")[:, 0:4], "normed_t")
+        others = to_columns(other_rows, 6, "centred")
+        gain_shift_bc = along_free_axis(others[:, 0:4], "centred")
+        pcg_bc = gain_shift_bc[:, 0:NP]
+        pcbeta_bc = gain_shift_bc[:, NP : 2 * NP]
+        pc_b_col = others[:, 4:6]
+        ln_g_col = keep.tile([P, PACK], F32)
+        nc.vector.tensor_copy(out=ln_g_col[:], in_=ln_g_raw[:])
+        ln_b_col = keep.tile([P, PACK], F32)
+        nc.vector.tensor_copy(out=ln_b_col[:], in_=ln_b_raw[:])
+
+        same_capsule = keep.tile([P, P // CAP_DIM], F32)
+        nc.vector.tensor_reduce(
+            out=same_capsule[:], in_=ident_f[:].rearrange("p (n q) -> p n q", q=CAP_DIM), axis=AXIS.X, op=ALU.add
+        )
+        centre = keep.tile([P, P], F32)
+        nc.vector.scalar_tensor_tensor(
+            out=centre[:].rearrange("p (n q) -> p n q", q=CAP_DIM),
+            in0=same_capsule[:].unsqueeze(2).to_broadcast([P, P // CAP_DIM, CAP_DIM]),
+            scalar=-1.0 / CAP_DIM,
+            in1=ident_f[:].rearrange("p (n q) -> p n q", q=CAP_DIM),
+            op0=ALU.mult,
+            op1=ALU.add,
+        )
+
+        pw_grouped = keep.tile([P, CAPS, CAP_DIM, PACK], BF16, align_bytes=64)
+        nc.scalar.copy(out=pw_grouped[:], in_=pw_sb[:].rearrange("p n (j q) -> p n q j", j=PACK))
+        pw_codes = keep.tile([P, NP], U32, align_bytes=64)
+        pw_plane = keep.tile([P, NP], U8, align_bytes=64)
+        nc.vector.quantize_mx(
+            out=pw_codes[:].bitcast(FP8X4),
+            scales=pw_plane[:],
+            in_=pw_grouped[:].rearrange("p n q j -> p (n q j)"),
+        )
+
+        for t in range(TILES):
+            h1_t = psum.tile([P, 2, P], F32, tag="h1_t")
+            words = h1_sb[:, t, :].bitcast(F32)
+            for u in range(2):
+                nc.tensor.transpose(h1_t[:, u, :], words[:, u : H1 // 2 : 2], ident_f[:])
+            h1_grouped = work.tile([P, P, PACK], BF16, align_bytes=64)
+            nc.vector.tensor_copy(out=h1_grouped[:].bitcast(F32), in_=h1_t[:].rearrange("p u r -> p r u"))
+            h1_codes = work.tile([P, P], U32, align_bytes=64)
+            h1_plane = work.tile([P, P], U8, align_bytes=64)
+            nc.vector.quantize_mx(
+                out=h1_codes[:].bitcast(FP8X4),
+                scales=h1_plane[:],
+                in_=h1_grouped[:].rearrange("p r k -> p (r k)"),
+            )
+
+            acc = psum.tile([P, E], F32, tag="acc", bufs=2)
+            nc.tensor.matmul_mx(
+                out=acc[:],
+                lhsT=h1_codes[:].bitcast(FP8X4),
+                lhsT_scale=h1_plane[:],
+                rhs=w2_codes[:].bitcast(FP8X4),
+                rhs_scale=w2_plane[:],
+                start=True,
+                stop=True,
+            )
+            z = work.tile([P, E], F32)
+            nc.vector.tensor_tensor(out=z[:], in0=acc[:], in1=b2_bc[:], op=ALU.add)
+            z_sum = work.tile([P, 1], F32)
+            nc.scalar.activation(out=z[:], in_=z[:], func=ACT.Relu, accum_out=z_sum[:])
+
+            squares = work.tile([P, E], BF16)
+            sq_sum = work.tile([P, 1], F32)
+            nc.scalar.activation(
+                out=squares[:], in_=z[:], func=ACT.Square, bias=z_sum[:], scale=-float(E), accum_out=sq_sum[:]
+            )
+            rstd = work.tile([P, 1], F32)
+            nc.scalar.activation(
+                out=rstd[:], in_=sq_sum[:], func=ACT.Abs_reciprocal_sqrt, bias=eps[:], scale=1.0 / float(E) ** 3
+            )
+            neg_mean = work.tile([P, 1], F32)
+            nc.vector.tensor_scalar(out=neg_mean[:], in0=z_sum[:], scalar1=-1.0 / E, scalar2=None, op0=ALU.mult)
+            normed = work.tile([P, E], F32)
+            nc.vector.tensor_scalar(
+                out=normed[:].rearrange("r (j p) -> r p j", j=PACK),
+                in0=z[:].rearrange("r (p j) -> r p j", j=PACK),
+                scalar1=neg_mean[:],
+                scalar2=rstd[:],
+                op0=ALU.add,
+                op1=ALU.mult,
+            )
+
+            normed_t = psum.tile([P, PACK, P], F32, tag="normed_t", bufs=2)
+            for j in range(PACK):
+                nc.tensor.transpose(normed_t[:, j, :], normed[:, P * j : P * (j + 1)], ident_f[:])
+            h_t = work.tile([P, PACK, P], BF16)
+            for j in range(PACK):
+                nc.scalar.activation(
+                    out=h_t[:, j, :],
+                    in_=normed_t[:, j, :],
+                    func=ACT.Identity,
+                    bias=ln_b_col[:, j : j + 1],
+                    scale=ln_g_col[:, j : j + 1],
+                )
+            h_grouped = work.tile([P, P, PACK], BF16, align_bytes=64)
+            nc.vector.tensor_copy(
+                out=h_grouped[:].rearrange("p (c x) j -> p c j x", x=4),
+                in_=h_t[:].rearrange("p j (c x) -> p c j x", x=4),
+            )
+            h_codes = work.tile([P, P], U32, align_bytes=64)
+            h_plane = work.tile([P, P], U8, align_bytes=64)
+            nc.vector.quantize_mx(
+                out=h_codes[:].bitcast(FP8X4),
+                scales=h_plane[:],
+                in_=h_grouped[:].rearrange("p r j -> p (r j)"),
+            )
+
+            prim_t = psum.tile([P, NP_TILES, P], F32, tag="prim_t")
+            biased_t = work.tile([P, NP_TILES, P], F32)
+            for c in range(NP_TILES):
+                cols = slice(P * c, P * (c + 1))
+                nc.tensor.matmul_mx(
+                    out=prim_t[:, c, :],
+                    lhsT=pw_codes[:, cols].bitcast(FP8X4),
+                    lhsT_scale=pw_plane[:, cols],
+                    rhs=h_codes[:].bitcast(FP8X4),
+                    rhs_scale=h_plane[:],
+                    start=True,
+                    stop=True,
+                )
+            for c in range(NP_TILES):
+                nc.scalar.activation(
+                    out=biased_t[:, c, :],
+                    in_=prim_t[:, c, :],
+                    func=ACT.Identity,
+                    bias=pc_b_col[:, c : c + 1],
+                    scale=1.0,
+                )
+
+            centred = psum.tile([P, CAPS, CAP_DIM], F32, tag="centred", bufs=2)
+            centred_flat = centred[:].rearrange("p n q -> p (n q)")
+            for c in range(NP_TILES):
+                nc.tensor.matmul(
+                    out=centred_flat[:, P * c : P * (c + 1)], lhsT=biased_t[:, c, :], rhs=centre[:], start=True, stop=True
+                )
+
+            cap_squares = work.tile([P, CAPS, CAP_DIM], F32)
+            nc.scalar.activation(out=cap_squares[:], in_=centred[:], func=ACT.Square)
+            cap_sq_sum = work.tile([P, CAPS], F32)
+            nc.vector.tensor_reduce(out=cap_sq_sum[:], in_=cap_squares[:], axis=AXIS.X, op=ALU.add)
+            cap_rstd = work.tile([P, CAPS], F32)
+            nc.scalar.activation(
+                out=cap_rstd[:], in_=cap_sq_sum[:], func=ACT.Abs_reciprocal_sqrt, bias=eps[:], scale=1.0 / CAP_DIM
+            )
+            result = work.tile([P, CAPS, CAP_DIM], F32)
+            nc.vector.tensor_tensor(
+                out=result[:],
+                in0=centred[:],
+                in1=cap_rstd[:].unsqueeze(2).to_broadcast([P, CAPS, CAP_DIM]),
+                op=ALU.mult,
+            )
+            result_flat = result[:].rearrange("p n q -> p (n q)")
+            nc.gpsimd.tensor_tensor(out=result_flat, in0=result_flat, in1=pcg_bc, op=ALU.mult)
+            nc.gpsimd.tensor_tensor(out=result_flat, in0=result_flat, in1=pcbeta_bc, op=ALU.add)
+            nc.sync.dma_start(out=out_rows[:, t, :], in_=result_flat)

@@ -18,9 +18,11 @@ PACK = 4
 B, H1, E = 2048, 512, 512
 CAPS, CAP_DIM = 32, 8
 NP = CAPS * CAP_DIM
-NP_TILES = NP // P
+HALVES = NP // P
 TILES = B // P
 EPS = 1e-5
+
+GROUPS = [[0], [1]] + [[t, t + 1] for t in range(2, TILES - 2, 2)] + [[TILES - 2], [TILES - 1]]
 
 FLOPS = 2 * B * H1 * E + 2 * B * E * NP
 
@@ -31,7 +33,7 @@ def tile_hotpatchcapsmodel_pa_kernel(
     nc = tc.nc
     with ExitStack() as ctx:
         keep = ctx.enter_context(tc.tile_pool(name="keep", bufs=1))
-        work = ctx.enter_context(tc.tile_pool(name="work", bufs=4))
+        work = ctx.enter_context(tc.tile_pool(name="work", bufs=3))
         psum = ctx.enter_context(tc.psum_pool(name="psum", bufs=1))
 
         h1_rows = h1.rearrange("(p t) k -> p t k", t=TILES)
@@ -39,12 +41,12 @@ def tile_hotpatchcapsmodel_pa_kernel(
 
         w2_plane = keep.tile([P, E], U8, align_bytes=64)
         nc.vector.memset(w2_plane[:].bitcast(I32), 0)
-        b2_rows = keep.tile([P, P], BF16)
-        nc.vector.memset(b2_rows[:], 0.0)
-        other_rows = keep.tile([P, P], BF16)
-        nc.vector.memset(other_rows[:], 0.0)
+        b2_rows = keep.tile([P, E], BF16)
+        nc.gpsimd.memset(b2_rows[:], 0.0)
         eps = keep.tile([P, 1], F32)
         nc.vector.memset(eps[:], EPS)
+        ones = keep.tile([P, P], BF16)
+        nc.vector.memset(ones[:], 1.0)
 
         h1_sb = keep.tile([P, TILES, H1], BF16)
         nc.sync.dma_start(out=h1_sb[:, 0:2, :], in_=h1_rows[:, 0:2, :])
@@ -58,159 +60,170 @@ def tile_hotpatchcapsmodel_pa_kernel(
                 out=w2_plane[32 * quadrant : 32 * quadrant + 4, :].bitcast(I32),
                 in_=W2_scales[0, 4 * quadrant : 4 * quadrant + 4, :].bitcast(I32),
             )
-        nc.sync.dma_start(out=b2_rows[0:4, :], in_=b2.rearrange("(j c) -> j c", c=P))
-        nc.sync.dma_start(out=other_rows[0:2, :], in_=pc_g.rearrange("(c n) q -> c (n q)", c=NP_TILES))
-        nc.sync.dma_start(out=other_rows[2:4, :], in_=pc_beta.rearrange("(c n) q -> c (n q)", c=NP_TILES))
-        nc.sync.dma_start(out=other_rows[4:6, :], in_=pc_b.rearrange("(c n) q -> c (n q)", c=NP_TILES))
+        nc.sync.dma_start(out=b2_rows[0:1, :], in_=b2.unsqueeze(0))
+        nc.sync.dma_start(out=h1_sb[:, 2:4, :], in_=h1_rows[:, 2:4, :])
         ln_g_raw = keep.tile([P, PACK], BF16)
         nc.sync.dma_start(out=ln_g_raw[:], in_=ln_g.rearrange("(p j) -> p j", j=PACK))
-        ln_b_raw = keep.tile([P, PACK], BF16)
-        nc.sync.dma_start(out=ln_b_raw[:], in_=ln_b.rearrange("(p j) -> p j", j=PACK))
-        pw_sb = keep.tile([P, CAPS, PACK * CAP_DIM], BF16)
-        nc.sync.dma_start(out=pw_sb[:], in_=pc_W.rearrange("n (p j) q -> p n (j q)", j=PACK))
-        for doubling in range(1, 4):
-            first = 2**doubling
-            nc.sync.dma_start(out=h1_sb[:, first : 2 * first, :], in_=h1_rows[:, first : 2 * first, :])
+        ln_b_col = keep.tile([P, PACK], BF16)
+        nc.sync.dma_start(out=ln_b_col[:], in_=ln_b.rearrange("(p j) -> p j", j=PACK))
+        pw_raw = keep.tile([P, CAPS, PACK * CAP_DIM], BF16)
+        nc.sync.dma_start(out=pw_raw[:], in_=pc_W.rearrange("n (p j) q -> p n (j q)", j=PACK))
+        pc_b_col = [keep.tile([P, 1], BF16, name="pc_b_col%d" % c) for c in range(HALVES)]
+        for c in range(HALVES):
+            rows = slice(CAPS // HALVES * c, CAPS // HALVES * (c + 1))
+            nc.sync.dma_start(out=pc_b_col[c][:], in_=pc_b[rows, :].rearrange("n q -> (n q)").unsqueeze(1))
+        nc.sync.dma_start(out=h1_sb[:, 4:8, :], in_=h1_rows[:, 4:8, :])
+        nc.sync.dma_start(out=h1_sb[:, 8:16, :], in_=h1_rows[:, 8:16, :])
+        pcg_bc = keep.tile([P, NP], BF16)
+        nc.sync.dma_start(out=pcg_bc[:], in_=pc_g.rearrange("n q -> (n q)").partition_broadcast(P))
+        pcbeta_bc = keep.tile([P, NP], BF16)
+        nc.sync.dma_start(out=pcbeta_bc[:], in_=pc_beta.rearrange("n q -> (n q)").partition_broadcast(P))
 
         warm = keep.tile([P, 1], F32)
         nc.scalar.activation(out=warm[:], in_=eps[:], func=ACT.Abs_reciprocal_sqrt)
 
-        ident_f = keep.tile([P, P], F32)
-        make_identity(nc, ident_f[:])
-        ident_b = keep.tile([P, P], BF16)
-        make_identity(nc, ident_b[:])
-
-        def to_columns(rows, count, tag):
-            rows_t = psum.tile([P, P], BF16, name="rows_t", tag=tag, bufs=2)
-            nc.tensor.transpose(rows_t[:], rows[:], ident_b[:])
-            columns = keep.tile([P, count], F32, name="columns_" + tag)
-            nc.vector.tensor_copy(out=columns[:], in_=rows_t[:, 0:count])
-            return columns
-
-        def along_free_axis(columns, tag):
-            repeated = keep.tile([P, 4, P], F32, name="repeated_" + tag)
-            nc.vector.tensor_copy(out=repeated[:], in_=columns.unsqueeze(2).to_broadcast([P, 4, P]))
-            spread = psum.tile([P, 4, P], F32, name="spread", tag=tag, bufs=2)
-            for k in range(4):
-                nc.tensor.transpose(spread[:, k, :], repeated[:, k, :], ident_f[:])
-            everywhere = keep.tile([P, 4 * P], F32, name="everywhere_" + tag)
-            nc.vector.tensor_copy(out=everywhere[:], in_=spread[:].rearrange("p k c -> p (k c)"))
-            return everywhere
-
-        b2_bc = along_free_axis(to_columns(b2_rows, 4, "normed_t")[:, 0:4], "normed_t")
-        others = to_columns(other_rows, 6, "centred")
-        gain_shift_bc = along_free_axis(others[:, 0:4], "centred")
-        pcg_bc = gain_shift_bc[:, 0:NP]
-        pcbeta_bc = gain_shift_bc[:, NP : 2 * NP]
-        pc_b_col = others[:, 4:6]
-        ln_g_col = keep.tile([P, PACK], F32)
-        nc.vector.tensor_copy(out=ln_g_col[:], in_=ln_g_raw[:])
-        ln_b_col = keep.tile([P, PACK], F32)
-        nc.vector.tensor_copy(out=ln_b_col[:], in_=ln_b_raw[:])
+        ident = keep.tile([P, P], F32)
+        make_identity(nc, ident[:])
 
         same_capsule = keep.tile([P, P // CAP_DIM], F32)
         nc.vector.tensor_reduce(
-            out=same_capsule[:], in_=ident_f[:].rearrange("p (n q) -> p n q", q=CAP_DIM), axis=AXIS.X, op=ALU.add
+            out=same_capsule[:], in_=ident[:].rearrange("p (n q) -> p n q", q=CAP_DIM), axis=AXIS.X, op=ALU.add
         )
         centre = keep.tile([P, P], F32)
         nc.vector.scalar_tensor_tensor(
             out=centre[:].rearrange("p (n q) -> p n q", q=CAP_DIM),
             in0=same_capsule[:].unsqueeze(2).to_broadcast([P, P // CAP_DIM, CAP_DIM]),
             scalar=-1.0 / CAP_DIM,
-            in1=ident_f[:].rearrange("p (n q) -> p n q", q=CAP_DIM),
+            in1=ident[:].rearrange("p (n q) -> p n q", q=CAP_DIM),
             op0=ALU.mult,
             op1=ALU.add,
         )
 
-        pw_grouped = keep.tile([P, CAPS, CAP_DIM, PACK], BF16, align_bytes=64)
-        nc.scalar.copy(out=pw_grouped[:], in_=pw_sb[:].rearrange("p n (j q) -> p n q j", j=PACK))
-        pw_codes = keep.tile([P, NP], U32, align_bytes=64)
-        pw_plane = keep.tile([P, NP], U8, align_bytes=64)
-        nc.vector.quantize_mx(
-            out=pw_codes[:].bitcast(FP8X4),
-            scales=pw_plane[:],
-            in_=pw_grouped[:].rearrange("p n q j -> p (n q j)"),
-        )
-
-        for t in range(TILES):
-            h1_t = psum.tile([P, 2, P], F32, tag="h1_t")
-            words = h1_sb[:, t, :].bitcast(F32)
-            for u in range(2):
-                nc.tensor.transpose(h1_t[:, u, :], words[:, u : H1 // 2 : 2], ident_f[:])
-            h1_grouped = work.tile([P, P, PACK], BF16, align_bytes=64)
-            nc.vector.tensor_copy(out=h1_grouped[:].bitcast(F32), in_=h1_t[:].rearrange("p u r -> p r u"))
-            h1_codes = work.tile([P, P], U32, align_bytes=64)
-            h1_plane = work.tile([P, P], U8, align_bytes=64)
+        def quantise_h1(group):
+            n = len(group)
+            h1_t = psum.tile([P, n, 2, P], F32, name="h1_t")
+            for i, t in enumerate(group):
+                words = h1_sb[:, t, :].bitcast(F32)
+                for u in range(2):
+                    nc.tensor.transpose(h1_t[:, i, u, :], words[:, u : H1 // 2 : 2], ident[:])
+            h1_grouped = work.tile([P, n, P, PACK], BF16, name="h1_grouped", align_bytes=64)
+            nc.vector.tensor_copy(out=h1_grouped[:].bitcast(F32), in_=h1_t[:].rearrange("p n u r -> p n r u"))
+            h1_codes = work.tile([P, n * P], U32, name="h1_codes", align_bytes=64)
+            h1_plane = work.tile([P, n * P], U8, name="h1_plane", align_bytes=64)
             nc.vector.quantize_mx(
                 out=h1_codes[:].bitcast(FP8X4),
                 scales=h1_plane[:],
-                in_=h1_grouped[:].rearrange("p r k -> p (r k)"),
+                in_=h1_grouped[:].rearrange("p n r k -> p (n r k)"),
             )
+            return h1_codes, h1_plane
 
-            acc = psum.tile([P, E], F32, tag="acc", bufs=2)
-            nc.tensor.matmul_mx(
-                out=acc[:],
-                lhsT=h1_codes[:].bitcast(FP8X4),
-                lhsT_scale=h1_plane[:],
-                rhs=w2_codes[:].bitcast(FP8X4),
-                rhs_scale=w2_plane[:],
-                start=True,
-                stop=True,
-            )
-            z = work.tile([P, E], F32)
-            nc.vector.tensor_tensor(out=z[:], in0=acc[:], in1=b2_bc[:], op=ALU.add)
-            z_sum = work.tile([P, 1], F32)
-            nc.scalar.activation(out=z[:], in_=z[:], func=ACT.Relu, accum_out=z_sum[:])
+        first_h1 = quantise_h1(GROUPS[0])
 
-            squares = work.tile([P, E], BF16)
-            sq_sum = work.tile([P, 1], F32)
-            nc.scalar.activation(
-                out=squares[:], in_=z[:], func=ACT.Square, bias=z_sum[:], scale=-float(E), accum_out=sq_sum[:]
+        b2_spread = psum.tile([P, E], F32, name="b2_spread", tag="acc", bufs=2)
+        nc.tensor.matmul(out=b2_spread[:], lhsT=ones[:], rhs=b2_rows[:], start=True, stop=True)
+        b2_bc = keep.tile([P, E], F32)
+        nc.scalar.copy(out=b2_bc[:], in_=b2_spread[:])
+
+        def prepare_pc_w():
+            grouped = keep.tile([P, CAPS, CAP_DIM, PACK], BF16, name="pw_grouped", align_bytes=64)
+            nc.scalar.copy(out=grouped[:], in_=pw_raw[:].rearrange("p n (j q) -> p n q j", j=PACK))
+            codes = keep.tile([P, NP], U32, name="pw_codes", align_bytes=64)
+            plane = keep.tile([P, NP], U8, name="pw_plane", align_bytes=64)
+            nc.vector.quantize_mx(
+                out=codes[:].bitcast(FP8X4), scales=plane[:], in_=grouped[:].rearrange("p n q j -> p (n q j)")
             )
-            rstd = work.tile([P, 1], F32)
+            return codes, plane
+
+        def front(group, h1_quantised):
+            n = len(group)
+            h1_codes, h1_plane = h1_quantised
+            z = []
+            z_sum = work.tile([P, n], F32, name="z_sum")
+            sq_sum = work.tile([P, n], F32, name="sq_sum")
+            for i in range(n):
+                rows = slice(P * i, P * (i + 1))
+                acc = psum.tile([P, E], F32, name="acc", tag="acc", bufs=2)
+                nc.tensor.matmul_mx(
+                    out=acc[:],
+                    lhsT=h1_codes[:, rows].bitcast(FP8X4),
+                    lhsT_scale=h1_plane[:, rows],
+                    rhs=w2_codes[:].bitcast(FP8X4),
+                    rhs_scale=w2_plane[:],
+                    start=True,
+                    stop=True,
+                )
+                z.append(work.tile([P, E], F32, name="z", bufs=5))
+                nc.vector.tensor_tensor(out=z[i][:], in0=acc[:], in1=b2_bc[:], op=ALU.add)
+            for i in range(n):
+                nc.scalar.activation(out=z[i][:], in_=z[i][:], func=ACT.Relu, accum_out=z_sum[:, i : i + 1])
+            neg_mean = work.tile([P, n], F32, name="neg_mean")
+            nc.vector.tensor_scalar(out=neg_mean[:], in0=z_sum[:], scalar1=-1.0 / E, scalar2=None, op0=ALU.mult)
+            for i in range(n):
+                squares = work.tile([P, E], BF16, name="squares")
+                nc.scalar.activation(
+                    out=squares[:],
+                    in_=z[i][:],
+                    func=ACT.Square,
+                    bias=z_sum[:, i : i + 1],
+                    scale=-float(E),
+                    accum_out=sq_sum[:, i : i + 1],
+                )
+            rstd = work.tile([P, n], F32, name="rstd")
             nc.scalar.activation(
                 out=rstd[:], in_=sq_sum[:], func=ACT.Abs_reciprocal_sqrt, bias=eps[:], scale=1.0 / float(E) ** 3
             )
-            neg_mean = work.tile([P, 1], F32)
-            nc.vector.tensor_scalar(out=neg_mean[:], in0=z_sum[:], scalar1=-1.0 / E, scalar2=None, op0=ALU.mult)
-            normed = work.tile([P, E], F32)
-            nc.vector.tensor_scalar(
-                out=normed[:].rearrange("r (j p) -> r p j", j=PACK),
-                in0=z[:].rearrange("r (p j) -> r p j", j=PACK),
-                scalar1=neg_mean[:],
-                scalar2=rstd[:],
-                op0=ALU.add,
-                op1=ALU.mult,
-            )
-
-            normed_t = psum.tile([P, PACK, P], F32, tag="normed_t", bufs=2)
-            for j in range(PACK):
-                nc.tensor.transpose(normed_t[:, j, :], normed[:, P * j : P * (j + 1)], ident_f[:])
-            h_t = work.tile([P, PACK, P], BF16)
-            for j in range(PACK):
-                nc.scalar.activation(
-                    out=h_t[:, j, :],
-                    in_=normed_t[:, j, :],
-                    func=ACT.Identity,
-                    bias=ln_b_col[:, j : j + 1],
-                    scale=ln_g_col[:, j : j + 1],
+            normed = []
+            for i in range(n):
+                normed.append(work.tile([P, E], F32, name="normed", bufs=4))
+                nc.vector.tensor_scalar(
+                    out=normed[i][:].rearrange("r (j p) -> r p j", j=PACK),
+                    in0=z[i][:].rearrange("r (p j) -> r p j", j=PACK),
+                    scalar1=neg_mean[:, i : i + 1],
+                    scalar2=rstd[:, i : i + 1],
+                    op0=ALU.add,
+                    op1=ALU.mult,
                 )
-            h_grouped = work.tile([P, P, PACK], BF16, align_bytes=64)
+            return normed
+
+        def middle(group, normed):
+            n = len(group)
+            h_t = work.tile([P, PACK, n * P], BF16, name="h_t")
+            for pair in range(2):
+                normed_t = psum.tile([P, 2, n * P], F32, name="normed_t", bufs=2)
+                for i in range(n):
+                    for j in range(2):
+                        k = 2 * pair + j
+                        nc.tensor.transpose(
+                            normed_t[:, j, P * i : P * (i + 1)], normed[i][:, P * k : P * (k + 1)], ident[:]
+                        )
+                for j in range(2):
+                    k = 2 * pair + j
+                    nc.scalar.activation(
+                        out=h_t[:, k, :],
+                        in_=normed_t[:, j, :],
+                        func=ACT.Identity,
+                        bias=ln_b_col[:, k : k + 1],
+                        scale=ln_g_col[:, k : k + 1],
+                    )
+            h_grouped = work.tile([P, n * P, PACK], BF16, name="h_grouped", align_bytes=64)
             nc.vector.tensor_copy(
                 out=h_grouped[:].rearrange("p (c x) j -> p c j x", x=4),
                 in_=h_t[:].rearrange("p j (c x) -> p c j x", x=4),
             )
-            h_codes = work.tile([P, P], U32, align_bytes=64)
-            h_plane = work.tile([P, P], U8, align_bytes=64)
+            h_codes = work.tile([P, n * P], U32, name="h_codes", align_bytes=64)
+            h_plane = work.tile([P, n * P], U8, name="h_plane", align_bytes=64)
             nc.vector.quantize_mx(
                 out=h_codes[:].bitcast(FP8X4),
                 scales=h_plane[:],
                 in_=h_grouped[:].rearrange("p r j -> p (r j)"),
             )
+            return h_codes, h_plane
 
-            prim_t = psum.tile([P, NP_TILES, P], F32, tag="prim_t")
-            biased_t = work.tile([P, NP_TILES, P], F32)
-            for c in range(NP_TILES):
+        def back(group, h_quantised):
+            n = len(group)
+            h_codes, h_plane = h_quantised
+            prim_t = psum.tile([P, HALVES, n * P], F32, name="prim_t")
+            for c in range(HALVES):
                 cols = slice(P * c, P * (c + 1))
                 nc.tensor.matmul_mx(
                     out=prim_t[:, c, :],
@@ -221,38 +234,49 @@ def tile_hotpatchcapsmodel_pa_kernel(
                     start=True,
                     stop=True,
                 )
-            for c in range(NP_TILES):
+            biased_t = work.tile([P, HALVES, n * P], F32, name="biased_t")
+            for c in range(HALVES):
                 nc.scalar.activation(
-                    out=biased_t[:, c, :],
-                    in_=prim_t[:, c, :],
-                    func=ACT.Identity,
-                    bias=pc_b_col[:, c : c + 1],
-                    scale=1.0,
+                    out=biased_t[:, c, :], in_=prim_t[:, c, :], func=ACT.Identity, bias=pc_b_col[c][:], scale=1.0
                 )
-
-            centred = psum.tile([P, CAPS, CAP_DIM], F32, tag="centred", bufs=2)
-            centred_flat = centred[:].rearrange("p n q -> p (n q)")
-            for c in range(NP_TILES):
-                nc.tensor.matmul(
-                    out=centred_flat[:, P * c : P * (c + 1)], lhsT=biased_t[:, c, :], rhs=centre[:], start=True, stop=True
-                )
-
-            cap_squares = work.tile([P, CAPS, CAP_DIM], F32)
+            centred = psum.tile([P, n * CAPS, CAP_DIM], F32, name="centred", bufs=2)
+            centred_flat = centred[:].rearrange("p m q -> p (m q)")
+            for i in range(n):
+                for c in range(HALVES):
+                    first = NP * i + P * c
+                    nc.tensor.matmul(
+                        out=centred_flat[:, first : first + P],
+                        lhsT=biased_t[:, c, P * i : P * (i + 1)],
+                        rhs=centre[:],
+                        start=True,
+                        stop=True,
+                    )
+            cap_squares = work.tile([P, n * CAPS, CAP_DIM], F32, name="cap_squares")
             nc.scalar.activation(out=cap_squares[:], in_=centred[:], func=ACT.Square)
-            cap_sq_sum = work.tile([P, CAPS], F32)
+            cap_sq_sum = work.tile([P, n * CAPS], F32, name="cap_sq_sum")
             nc.vector.tensor_reduce(out=cap_sq_sum[:], in_=cap_squares[:], axis=AXIS.X, op=ALU.add)
-            cap_rstd = work.tile([P, CAPS], F32)
+            cap_rstd = work.tile([P, n * CAPS], F32, name="cap_rstd")
             nc.scalar.activation(
                 out=cap_rstd[:], in_=cap_sq_sum[:], func=ACT.Abs_reciprocal_sqrt, bias=eps[:], scale=1.0 / CAP_DIM
             )
-            result = work.tile([P, CAPS, CAP_DIM], F32)
+            result = work.tile([P, n, NP], F32, name="result")
             nc.vector.tensor_tensor(
-                out=result[:],
+                out=result[:].rearrange("p n (m q) -> p (n m) q", q=CAP_DIM),
                 in0=centred[:],
-                in1=cap_rstd[:].unsqueeze(2).to_broadcast([P, CAPS, CAP_DIM]),
+                in1=cap_rstd[:].unsqueeze(2).to_broadcast([P, n * CAPS, CAP_DIM]),
                 op=ALU.mult,
             )
-            result_flat = result[:].rearrange("p n q -> p (n q)")
-            nc.gpsimd.tensor_tensor(out=result_flat, in0=result_flat, in1=pcg_bc, op=ALU.mult)
-            nc.gpsimd.tensor_tensor(out=result_flat, in0=result_flat, in1=pcbeta_bc, op=ALU.add)
-            nc.sync.dma_start(out=out_rows[:, t, :], in_=result_flat)
+            engine = nc.vector if group[-1] == TILES - 1 else nc.gpsimd
+            gain = pcg_bc[:].unsqueeze(1).to_broadcast([P, n, NP])
+            shift = pcbeta_bc[:].unsqueeze(1).to_broadcast([P, n, NP])
+            engine.tensor_tensor(out=result[:], in0=result[:], in1=gain, op=ALU.mult)
+            engine.tensor_tensor(out=result[:], in0=result[:], in1=shift, op=ALU.add)
+            nc.sync.dma_start(out=out_rows[:, group[0] : group[0] + n, :], in_=result[:])
+
+        ln_g_col = keep.tile([P, PACK], F32)
+        nc.vector.tensor_copy(out=ln_g_col[:], in_=ln_g_raw[:])
+        for g, group in enumerate(GROUPS):
+            normed = front(group, first_h1 if g == 0 else quantise_h1(group))
+            if g == 0:
+                pw_codes, pw_plane = prepare_pc_w()
+            back(group, middle(group, normed))

@@ -22,8 +22,6 @@ HALVES = NP // P
 TILES = B // P
 EPS = 1e-5
 
-GROUPS = [[0], [1]] + [[t, t + 1] for t in range(2, TILES - 2, 2)] + [[TILES - 2], [TILES - 1]]
-
 FLOPS = 2 * B * H1 * E + 2 * B * E * NP
 
 
@@ -33,14 +31,14 @@ def tile_hotpatchcapsmodel_pa_kernel(
     nc = tc.nc
     with ExitStack() as ctx:
         keep = ctx.enter_context(tc.tile_pool(name="keep", bufs=1))
-        work = ctx.enter_context(tc.tile_pool(name="work", bufs=3))
+        work = ctx.enter_context(tc.tile_pool(name="work", bufs=4))
         psum = ctx.enter_context(tc.psum_pool(name="psum", bufs=1))
 
         h1_rows = h1.rearrange("(p t) k -> p t k", t=TILES)
         out_rows = out.rearrange("(p t) n q -> p t (n q)", t=TILES)
 
-        w2_plane = keep.tile([P, E], U8, align_bytes=64)
-        nc.vector.memset(w2_plane[:].bitcast(I32), 0)
+        w2_plane_raw = keep.tile([P, E], U8, align_bytes=64)
+        nc.vector.memset(w2_plane_raw[:].bitcast(I32), 0)
         b2_rows = keep.tile([P, E], BF16)
         nc.gpsimd.memset(b2_rows[:], 0.0)
         eps = keep.tile([P, 1], F32)
@@ -49,25 +47,25 @@ def tile_hotpatchcapsmodel_pa_kernel(
         nc.vector.memset(ones[:], 1.0)
 
         h1_sb = keep.tile([P, TILES, H1], BF16)
-        nc.sync.dma_start(out=h1_sb[:, 0:2, :], in_=h1_rows[:, 0:2, :])
-        w2_codes = keep.tile([P, E], U32, align_bytes=64)
+        nc.sync.dma_start(out=h1_sb[:, 0:1, :], in_=h1_rows[:, 0:1, :])
+        w2_codes_raw = keep.tile([P, E], U32, align_bytes=64)
         nc.sync.dma_start(
-            out=w2_codes[:].bitcast(I32),
+            out=w2_codes_raw[:].bitcast(I32),
             in_=W2_words[0].rearrange("p n t -> p (n t)").bitcast(I32),
         )
         for quadrant in range(4):
             nc.sync.dma_start(
-                out=w2_plane[32 * quadrant : 32 * quadrant + 4, :].bitcast(I32),
+                out=w2_plane_raw[32 * quadrant : 32 * quadrant + 4, :].bitcast(I32),
                 in_=W2_scales[0, 4 * quadrant : 4 * quadrant + 4, :].bitcast(I32),
             )
         nc.sync.dma_start(out=b2_rows[0:1, :], in_=b2.unsqueeze(0))
-        nc.sync.dma_start(out=h1_sb[:, 2:4, :], in_=h1_rows[:, 2:4, :])
+        nc.sync.dma_start(out=h1_sb[:, 1:4, :], in_=h1_rows[:, 1:4, :])
+        pw_raw = keep.tile([P, CAPS, PACK * CAP_DIM], BF16)
+        nc.sync.dma_start(out=pw_raw[:], in_=pc_W.rearrange("n (p j) q -> p n (j q)", j=PACK))
         ln_g_raw = keep.tile([P, PACK], BF16)
         nc.sync.dma_start(out=ln_g_raw[:], in_=ln_g.rearrange("(p j) -> p j", j=PACK))
         ln_b_col = keep.tile([P, PACK], BF16)
         nc.sync.dma_start(out=ln_b_col[:], in_=ln_b.rearrange("(p j) -> p j", j=PACK))
-        pw_raw = keep.tile([P, CAPS, PACK * CAP_DIM], BF16)
-        nc.sync.dma_start(out=pw_raw[:], in_=pc_W.rearrange("n (p j) q -> p n (j q)", j=PACK))
         pc_b_col = [keep.tile([P, 1], BF16, name="pc_b_col%d" % c) for c in range(HALVES)]
         for c in range(HALVES):
             rows = slice(CAPS // HALVES * c, CAPS // HALVES * (c + 1))
@@ -99,184 +97,265 @@ def tile_hotpatchcapsmodel_pa_kernel(
             op1=ALU.add,
         )
 
-        def quantise_h1(group):
-            n = len(group)
-            h1_t = psum.tile([P, n, 2, P], F32, name="h1_t")
-            for i, t in enumerate(group):
-                words = h1_sb[:, t, :].bitcast(F32)
-                for u in range(2):
-                    nc.tensor.transpose(h1_t[:, i, u, :], words[:, u : H1 // 2 : 2], ident[:])
-            h1_grouped = work.tile([P, n, P, PACK], BF16, name="h1_grouped", align_bytes=64)
-            nc.vector.tensor_copy(out=h1_grouped[:].bitcast(F32), in_=h1_t[:].rearrange("p n u r -> p n r u"))
-            h1_codes = work.tile([P, n * P], U32, name="h1_codes", align_bytes=64)
-            h1_plane = work.tile([P, n * P], U8, name="h1_plane", align_bytes=64)
-            nc.vector.quantize_mx(
-                out=h1_codes[:].bitcast(FP8X4),
-                scales=h1_plane[:],
-                in_=h1_grouped[:].rearrange("p n r k -> p (n r k)"),
-            )
-            return h1_codes, h1_plane
-
-        first_h1 = quantise_h1(GROUPS[0])
-
-        b2_spread = psum.tile([P, E], F32, name="b2_spread", tag="acc", bufs=2)
-        nc.tensor.matmul(out=b2_spread[:], lhsT=ones[:], rhs=b2_rows[:], start=True, stop=True)
+        w2_codes = keep.tile([P, E], U32, align_bytes=64)
+        w2_plane = keep.tile([P, E], U8, align_bytes=64)
         b2_bc = keep.tile([P, E], F32)
-        nc.scalar.copy(out=b2_bc[:], in_=b2_spread[:])
+        ln_g_col = keep.tile([P, PACK], F32)
+        pw_grouped = keep.tile([P, CAPS, CAP_DIM, PACK], BF16, align_bytes=64)
+        pw_codes = keep.tile([P, NP], U32, align_bytes=64)
+        pw_plane = keep.tile([P, NP], U8, align_bytes=64)
 
-        def prepare_pc_w():
-            grouped = keep.tile([P, CAPS, CAP_DIM, PACK], BF16, name="pw_grouped", align_bytes=64)
-            nc.scalar.copy(out=grouped[:], in_=pw_raw[:].rearrange("p n (j q) -> p n q j", j=PACK))
-            codes = keep.tile([P, NP], U32, name="pw_codes", align_bytes=64)
-            plane = keep.tile([P, NP], U8, name="pw_plane", align_bytes=64)
-            nc.vector.quantize_mx(
-                out=codes[:].bitcast(FP8X4), scales=plane[:], in_=grouped[:].rearrange("p n q j -> p (n q j)")
-            )
-            return codes, plane
-
-        def front(group, h1_quantised):
-            n = len(group)
-            h1_codes, h1_plane = h1_quantised
-            z = []
-            z_sum = work.tile([P, n], F32, name="z_sum")
-            sq_sum = work.tile([P, n], F32, name="sq_sum")
-            for i in range(n):
-                rows = slice(P * i, P * (i + 1))
-                acc = psum.tile([P, E], F32, name="acc", tag="acc", bufs=2)
-                nc.tensor.matmul_mx(
-                    out=acc[:],
-                    lhsT=h1_codes[:, rows].bitcast(FP8X4),
-                    lhsT_scale=h1_plane[:, rows],
-                    rhs=w2_codes[:].bitcast(FP8X4),
-                    rhs_scale=w2_plane[:],
-                    start=True,
-                    stop=True,
-                )
-                z.append(work.tile([P, E], F32, name="z", bufs=5))
-                nc.vector.tensor_tensor(out=z[i][:], in0=acc[:], in1=b2_bc[:], op=ALU.add)
-            for i in range(n):
-                nc.scalar.activation(out=z[i][:], in_=z[i][:], func=ACT.Relu, accum_out=z_sum[:, i : i + 1])
-            neg_mean = work.tile([P, n], F32, name="neg_mean")
-            nc.vector.tensor_scalar(out=neg_mean[:], in0=z_sum[:], scalar1=-1.0 / E, scalar2=None, op0=ALU.mult)
-            for i in range(n):
-                squares = work.tile([P, E], BF16, name="squares")
-                nc.scalar.activation(
-                    out=squares[:],
-                    in_=z[i][:],
-                    func=ACT.Square,
-                    bias=z_sum[:, i : i + 1],
-                    scale=-float(E),
-                    accum_out=sq_sum[:, i : i + 1],
-                )
-            rstd = work.tile([P, n], F32, name="rstd")
-            nc.scalar.activation(
-                out=rstd[:], in_=sq_sum[:], func=ACT.Abs_reciprocal_sqrt, bias=eps[:], scale=1.0 / float(E) ** 3
-            )
-            normed = []
-            for i in range(n):
-                normed.append(work.tile([P, E], F32, name="normed", bufs=4))
-                nc.vector.tensor_scalar(
-                    out=normed[i][:].rearrange("r (j p) -> r p j", j=PACK),
-                    in0=z[i][:].rearrange("r (p j) -> r p j", j=PACK),
-                    scalar1=neg_mean[:, i : i + 1],
-                    scalar2=rstd[:, i : i + 1],
-                    op0=ALU.add,
-                    op1=ALU.mult,
-                )
-            return normed
-
-        def middle(group, normed):
-            n = len(group)
-            h_t = work.tile([P, PACK, n * P], BF16, name="h_t")
-            for pair in range(2):
-                normed_t = psum.tile([P, 2, n * P], F32, name="normed_t", bufs=2)
-                for i in range(n):
-                    for j in range(2):
-                        k = 2 * pair + j
-                        nc.tensor.transpose(
-                            normed_t[:, j, P * i : P * (i + 1)], normed[i][:, P * k : P * (k + 1)], ident[:]
-                        )
-                for j in range(2):
-                    k = 2 * pair + j
-                    nc.scalar.activation(
-                        out=h_t[:, k, :],
-                        in_=normed_t[:, j, :],
-                        func=ACT.Identity,
-                        bias=ln_b_col[:, k : k + 1],
-                        scale=ln_g_col[:, k : k + 1],
-                    )
-            h_grouped = work.tile([P, n * P, PACK], BF16, name="h_grouped", align_bytes=64)
+        def order_w2_codes():
             nc.vector.tensor_copy(
-                out=h_grouped[:].rearrange("p (c x) j -> p c j x", x=4),
-                in_=h_t[:].rearrange("p j (c x) -> p c j x", x=4),
+                out=w2_codes[:].bitcast(I32).rearrange("k (j p) -> k p j", j=PACK),
+                in_=w2_codes_raw[:].bitcast(I32).rearrange("k (p j) -> k p j", j=PACK),
             )
-            h_codes = work.tile([P, n * P], U32, name="h_codes", align_bytes=64)
-            h_plane = work.tile([P, n * P], U8, name="h_plane", align_bytes=64)
-            nc.vector.quantize_mx(
-                out=h_codes[:].bitcast(FP8X4),
-                scales=h_plane[:],
-                in_=h_grouped[:].rearrange("p r j -> p (r j)"),
-            )
-            return h_codes, h_plane
 
-        def back(group, h_quantised):
-            n = len(group)
-            h_codes, h_plane = h_quantised
-            prim_t = psum.tile([P, HALVES, n * P], F32, name="prim_t")
+        def order_w2_plane():
+            nc.vector.tensor_copy(
+                out=w2_plane[:].rearrange("k (j p) -> k p j", j=PACK),
+                in_=w2_plane_raw[:].rearrange("k (p j) -> k p j", j=PACK),
+            )
+
+        def spread_b2():
+            b2_spread = psum.tile([P, E], F32, name="b2_spread", tag="acc", bufs=2)
+            nc.tensor.matmul(out=b2_spread[:], lhsT=ones[:], rhs=b2_rows[:], start=True, stop=True)
+            nc.scalar.copy(
+                out=b2_bc[:].rearrange("r (j p) -> r j p", j=PACK),
+                in_=b2_spread[:].rearrange("r (p j) -> r j p", j=PACK),
+            )
+
+        def interleave_pc_w():
+            nc.gpsimd.tensor_copy(out=ln_g_col[:], in_=ln_g_raw[:])
+            nc.gpsimd.tensor_scalar(
+                out=pw_grouped[:],
+                in0=pw_raw[:].rearrange("p n (j q) -> p n q j", j=PACK),
+                scalar1=1.0,
+                scalar2=0.0,
+                op0=ALU.mult,
+                op1=ALU.add,
+            )
+
+        def quantise_pc_w():
+            nc.vector.quantize_mx(
+                out=pw_codes[:].bitcast(FP8X4), scales=pw_plane[:], in_=pw_grouped[:].rearrange("p n q j -> p (n q j)")
+            )
+
+        def transpose_h1(t, s):
+            s["h1_t"] = psum.tile([P, 2, P], F32, name="h1_t")
+            words = h1_sb[:, t, :].bitcast(F32)
+            for u in range(2):
+                nc.tensor.transpose(s["h1_t"][:, u, :], words[:, u : H1 // 2 : 2], ident[:])
+
+        def interleave_h1(t, s):
+            s["h1_grouped"] = work.tile([P, P, PACK], BF16, name="h1_grouped", align_bytes=64)
+            nc.vector.tensor_copy(out=s["h1_grouped"][:].bitcast(F32), in_=s["h1_t"][:].rearrange("p u r -> p r u"))
+
+        def quantise_h1(t, s):
+            s["h1_codes"] = work.tile([P, P], U32, name="h1_codes", align_bytes=64)
+            s["h1_plane"] = work.tile([P, P], U8, name="h1_plane", align_bytes=64)
+            nc.vector.quantize_mx(
+                out=s["h1_codes"][:].bitcast(FP8X4),
+                scales=s["h1_plane"][:],
+                in_=s["h1_grouped"][:].rearrange("p r k -> p (r k)"),
+            )
+
+        def first_product(t, s):
+            s["acc"] = psum.tile([P, E], F32, name="acc", tag="acc", bufs=2)
+            nc.tensor.matmul_mx(
+                out=s["acc"][:],
+                lhsT=s["h1_codes"][:].bitcast(FP8X4),
+                lhsT_scale=s["h1_plane"][:],
+                rhs=w2_codes[:].bitcast(FP8X4),
+                rhs_scale=w2_plane[:],
+                start=True,
+                stop=True,
+            )
+
+        def add_b2(t, s):
+            s["z"] = work.tile([P, E], F32, name="z")
+            nc.vector.tensor_tensor(out=s["z"][:], in0=s["acc"][:], in1=b2_bc[:], op=ALU.add)
+
+        def relu(t, s):
+            s["z_sum"] = work.tile([P, 1], F32, name="z_sum")
+            nc.scalar.activation(out=s["z"][:], in_=s["z"][:], func=ACT.Relu, accum_out=s["z_sum"][:])
+
+        def mean(t, s):
+            s["neg_mean"] = work.tile([P, 1], F32, name="neg_mean")
+            nc.gpsimd.tensor_scalar(
+                out=s["neg_mean"][:], in0=s["z_sum"][:], scalar1=-1.0 / E, scalar2=None, op0=ALU.mult
+            )
+
+        def squares(t, s):
+            s["sq_sum"] = work.tile([P, 1], F32, name="sq_sum")
+            unused = work.tile([P, E], BF16, name="unused")
+            nc.scalar.activation(
+                out=unused[:],
+                in_=s["z"][:],
+                func=ACT.Square,
+                bias=s["z_sum"][:],
+                scale=-float(E),
+                accum_out=s["sq_sum"][:],
+            )
+
+        def rstd(t, s):
+            s["rstd"] = work.tile([P, 1], F32, name="rstd")
+            nc.scalar.activation(
+                out=s["rstd"][:], in_=s["sq_sum"][:], func=ACT.Abs_reciprocal_sqrt, bias=eps[:], scale=1.0 / float(E) ** 3
+            )
+
+        def normalise(t, s):
+            s["normed"] = work.tile([P, E], F32, name="normed")
+            nc.vector.tensor_scalar(
+                out=s["normed"][:],
+                in0=s["z"][:],
+                scalar1=s["neg_mean"][:],
+                scalar2=s["rstd"][:],
+                op0=ALU.add,
+                op1=ALU.mult,
+            )
+
+        def transpose_h(t, s):
+            s["normed_t"] = psum.tile([P, PACK, P], F32, name="normed_t", bufs=2)
+            for j in range(PACK):
+                nc.tensor.transpose(s["normed_t"][:, j, :], s["normed"][:, P * j : P * (j + 1)], ident[:])
+
+        def affine(t, s):
+            s["h_t"] = work.tile([P, PACK, P], BF16, name="h_t")
+            for j in range(PACK):
+                nc.scalar.activation(
+                    out=s["h_t"][:, j, :],
+                    in_=s["normed_t"][:, j, :],
+                    func=ACT.Identity,
+                    bias=ln_b_col[:, j : j + 1],
+                    scale=ln_g_col[:, j : j + 1],
+                )
+
+        def interleave_h(t, s):
+            s["h_grouped"] = work.tile([P, P, PACK], BF16, name="h_grouped", align_bytes=64)
+            nc.vector.tensor_copy(
+                out=s["h_grouped"][:].rearrange("p (c x) j -> p c j x", x=4),
+                in_=s["h_t"][:].rearrange("p j (c x) -> p c j x", x=4),
+            )
+
+        def quantise_h(t, s):
+            s["h_codes"] = work.tile([P, P], U32, name="h_codes", align_bytes=64)
+            s["h_plane"] = work.tile([P, P], U8, name="h_plane", align_bytes=64)
+            nc.vector.quantize_mx(
+                out=s["h_codes"][:].bitcast(FP8X4),
+                scales=s["h_plane"][:],
+                in_=s["h_grouped"][:].rearrange("p r j -> p (r j)"),
+            )
+
+        def second_product(t, s):
+            s["prim_t"] = psum.tile([P, HALVES, P], F32, name="prim_t")
             for c in range(HALVES):
                 cols = slice(P * c, P * (c + 1))
                 nc.tensor.matmul_mx(
-                    out=prim_t[:, c, :],
+                    out=s["prim_t"][:, c, :],
                     lhsT=pw_codes[:, cols].bitcast(FP8X4),
                     lhsT_scale=pw_plane[:, cols],
-                    rhs=h_codes[:].bitcast(FP8X4),
-                    rhs_scale=h_plane[:],
+                    rhs=s["h_codes"][:].bitcast(FP8X4),
+                    rhs_scale=s["h_plane"][:],
                     start=True,
                     stop=True,
                 )
-            biased_t = work.tile([P, HALVES, n * P], F32, name="biased_t")
+
+        def add_pc_b(t, s):
+            s["biased_t"] = work.tile([P, HALVES, P], F32, name="biased_t")
             for c in range(HALVES):
                 nc.scalar.activation(
-                    out=biased_t[:, c, :], in_=prim_t[:, c, :], func=ACT.Identity, bias=pc_b_col[c][:], scale=1.0
+                    out=s["biased_t"][:, c, :],
+                    in_=s["prim_t"][:, c, :],
+                    func=ACT.Identity,
+                    bias=pc_b_col[c][:],
+                    scale=1.0,
                 )
-            centred = psum.tile([P, n * CAPS, CAP_DIM], F32, name="centred", bufs=2)
-            centred_flat = centred[:].rearrange("p m q -> p (m q)")
-            for i in range(n):
-                for c in range(HALVES):
-                    first = NP * i + P * c
-                    nc.tensor.matmul(
-                        out=centred_flat[:, first : first + P],
-                        lhsT=biased_t[:, c, P * i : P * (i + 1)],
-                        rhs=centre[:],
-                        start=True,
-                        stop=True,
-                    )
-            cap_squares = work.tile([P, n * CAPS, CAP_DIM], F32, name="cap_squares")
-            nc.scalar.activation(out=cap_squares[:], in_=centred[:], func=ACT.Square)
-            cap_sq_sum = work.tile([P, n * CAPS], F32, name="cap_sq_sum")
-            nc.vector.tensor_reduce(out=cap_sq_sum[:], in_=cap_squares[:], axis=AXIS.X, op=ALU.add)
-            cap_rstd = work.tile([P, n * CAPS], F32, name="cap_rstd")
+
+        def take_means_off(t, s):
+            s["centred"] = psum.tile([P, CAPS, CAP_DIM], F32, name="centred", bufs=2)
+            flat = s["centred"][:].rearrange("p m q -> p (m q)")
+            for c in range(HALVES):
+                nc.tensor.matmul(
+                    out=flat[:, P * c : P * (c + 1)],
+                    lhsT=s["biased_t"][:, c, :],
+                    rhs=centre[:],
+                    start=True,
+                    stop=True,
+                )
+
+        def capsule_squares(t, s):
+            s["cap_squares"] = work.tile([P, CAPS, CAP_DIM], F32, name="cap_squares")
+            nc.scalar.activation(out=s["cap_squares"][:], in_=s["centred"][:], func=ACT.Square)
+
+        def capsule_sums(t, s):
+            s["cap_sq_sum"] = work.tile([P, CAPS], F32, name="cap_sq_sum")
+            nc.vector.tensor_reduce(out=s["cap_sq_sum"][:], in_=s["cap_squares"][:], axis=AXIS.X, op=ALU.add)
+
+        def capsule_rstd(t, s):
+            s["cap_rstd"] = work.tile([P, CAPS], F32, name="cap_rstd")
             nc.scalar.activation(
-                out=cap_rstd[:], in_=cap_sq_sum[:], func=ACT.Abs_reciprocal_sqrt, bias=eps[:], scale=1.0 / CAP_DIM
+                out=s["cap_rstd"][:],
+                in_=s["cap_sq_sum"][:],
+                func=ACT.Abs_reciprocal_sqrt,
+                bias=eps[:],
+                scale=1.0 / CAP_DIM,
             )
-            result = work.tile([P, n, NP], F32, name="result")
+
+        def scale_capsules(t, s):
+            s["result"] = work.tile([P, NP], F32, name="result")
             nc.vector.tensor_tensor(
-                out=result[:].rearrange("p n (m q) -> p (n m) q", q=CAP_DIM),
-                in0=centred[:],
-                in1=cap_rstd[:].unsqueeze(2).to_broadcast([P, n * CAPS, CAP_DIM]),
+                out=s["result"][:].rearrange("p (m q) -> p m q", q=CAP_DIM),
+                in0=s["centred"][:],
+                in1=s["cap_rstd"][:].unsqueeze(2).to_broadcast([P, CAPS, CAP_DIM]),
                 op=ALU.mult,
             )
-            engine = nc.vector if group[-1] == TILES - 1 else nc.gpsimd
-            gain = pcg_bc[:].unsqueeze(1).to_broadcast([P, n, NP])
-            shift = pcbeta_bc[:].unsqueeze(1).to_broadcast([P, n, NP])
-            engine.tensor_tensor(out=result[:], in0=result[:], in1=gain, op=ALU.mult)
-            engine.tensor_tensor(out=result[:], in0=result[:], in1=shift, op=ALU.add)
-            nc.sync.dma_start(out=out_rows[:, group[0] : group[0] + n, :], in_=result[:])
 
-        ln_g_col = keep.tile([P, PACK], F32)
-        nc.vector.tensor_copy(out=ln_g_col[:], in_=ln_g_raw[:])
-        for g, group in enumerate(GROUPS):
-            normed = front(group, first_h1 if g == 0 else quantise_h1(group))
-            if g == 0:
-                pw_codes, pw_plane = prepare_pc_w()
-            back(group, middle(group, normed))
+        def gain_and_shift(t, s):
+            engine = nc.vector if t == TILES - 1 else nc.gpsimd
+            engine.tensor_tensor(out=s["result"][:], in0=s["result"][:], in1=pcg_bc[:], op=ALU.mult)
+            engine.tensor_tensor(out=s["result"][:], in0=s["result"][:], in1=pcbeta_bc[:], op=ALU.add)
+
+        def store(t, s):
+            nc.sync.dma_start(out=out_rows[:, t, :], in_=s["result"][:])
+
+        STEP = [
+            (scale_capsules, 9),
+            (gain_and_shift, 9),
+            (store, 9),
+            (interleave_h1, 1),
+            (rstd, 4),
+            (take_means_off, 8),
+            (first_product, 2),
+            (second_product, 7),
+            (affine, 6),
+            (capsule_squares, 8),
+            (transpose_h, 5),
+            (add_b2, 2),
+            (add_pc_b, 7),
+            (capsule_sums, 8),
+            (squares, 3),
+            (quantise_h1, 1),
+            (mean, 3),
+            (interleave_h, 6),
+            (capsule_rstd, 8),
+            (transpose_h1, 0),
+            (normalise, 4),
+            (quantise_h, 6),
+            (relu, 2),
+        ]
+        state = [{} for t in range(TILES)]
+        with tc.manual_schedule():
+            for step in range(TILES + 9):
+                if step == 1:
+                    spread_b2()
+                    order_w2_codes()
+                    interleave_pc_w()
+                if step == 2:
+                    order_w2_plane()
+                if step == 4:
+                    quantise_pc_w()
+                for stage, behind in STEP:
+                    t = step - behind
+                    if 0 <= t < TILES:
+                        stage(t, state[t])

@@ -118,7 +118,7 @@ def tile_hotpatchcapsmodel_pa_kernel(
             )
 
         def spread_b2():
-            b2_spread = psum.tile([P, E], F32, name="b2_spread", tag="acc", bufs=2)
+            b2_spread = psum.tile([P, E], F32, name="b2_spread", tag="acc")
             nc.tensor.matmul(out=b2_spread[:], lhsT=ones[:], rhs=b2_rows[:], start=True, stop=True)
             nc.scalar.copy(
                 out=b2_bc[:].rearrange("r (j p) -> r j p", j=PACK),
@@ -161,7 +161,7 @@ def tile_hotpatchcapsmodel_pa_kernel(
             )
 
         def first_product(t, s):
-            s["acc"] = psum.tile([P, E], F32, name="acc", tag="acc", bufs=2)
+            s["acc"] = psum.tile([P, E], F32, name="acc", tag="acc")
             nc.tensor.matmul_mx(
                 out=s["acc"][:],
                 lhsT=s["h1_codes"][:].bitcast(FP8X4),
@@ -180,12 +180,6 @@ def tile_hotpatchcapsmodel_pa_kernel(
             s["z_sum"] = work.tile([P, 1], F32, name="z_sum")
             nc.scalar.activation(out=s["z"][:], in_=s["z"][:], func=ACT.Relu, accum_out=s["z_sum"][:])
 
-        def mean(t, s):
-            s["neg_mean"] = work.tile([P, 1], F32, name="neg_mean")
-            nc.gpsimd.tensor_scalar(
-                out=s["neg_mean"][:], in0=s["z_sum"][:], scalar1=-1.0 / E, scalar2=None, op0=ALU.mult
-            )
-
         def squares(t, s):
             s["sq_sum"] = work.tile([P, 1], F32, name="sq_sum")
             unused = work.tile([P, E], BF16, name="unused")
@@ -199,6 +193,8 @@ def tile_hotpatchcapsmodel_pa_kernel(
             )
 
         def rstd(t, s):
+            s["neg_mean"] = work.tile([P, 1], F32, name="neg_mean")
+            nc.scalar.mul(out=s["neg_mean"][:], in_=s["z_sum"][:], mul=-1.0 / E)
             s["rstd"] = work.tile([P, 1], F32, name="rstd")
             nc.scalar.activation(
                 out=s["rstd"][:], in_=s["sq_sum"][:], func=ACT.Abs_reciprocal_sqrt, bias=eps[:], scale=1.0 / float(E) ** 3
@@ -248,11 +244,12 @@ def tile_hotpatchcapsmodel_pa_kernel(
             )
 
         def second_product(t, s):
-            s["prim_t"] = psum.tile([P, HALVES, P], F32, name="prim_t")
+            s["prim_t"] = []
             for c in range(HALVES):
+                s["prim_t"].append(psum.tile([P, P], F32, name="prim_t", bufs=HALVES))
                 cols = slice(P * c, P * (c + 1))
                 nc.tensor.matmul_mx(
-                    out=s["prim_t"][:, c, :],
+                    out=s["prim_t"][c][:],
                     lhsT=pw_codes[:, cols].bitcast(FP8X4),
                     lhsT_scale=pw_plane[:, cols],
                     rhs=s["h_codes"][:].bitcast(FP8X4),
@@ -262,15 +259,13 @@ def tile_hotpatchcapsmodel_pa_kernel(
                 )
 
         def add_pc_b(t, s):
-            s["biased_t"] = work.tile([P, HALVES, P], F32, name="biased_t")
-            for c in range(HALVES):
-                nc.scalar.activation(
-                    out=s["biased_t"][:, c, :],
-                    in_=s["prim_t"][:, c, :],
-                    func=ACT.Identity,
-                    bias=pc_b_col[c][:],
-                    scale=1.0,
-                )
+            s["biased_t"] = [work.tile([P, P], F32, name="biased_t%d" % c) for c in range(HALVES)]
+            nc.scalar.activation(
+                out=s["biased_t"][0][:], in_=s["prim_t"][0][:], func=ACT.Identity, bias=pc_b_col[0][:], scale=1.0
+            )
+            nc.vector.tensor_scalar(
+                out=s["biased_t"][1][:], in0=s["prim_t"][1][:], scalar1=pc_b_col[1][:], scalar2=None, op0=ALU.add
+            )
 
         def take_means_off(t, s):
             s["centred"] = psum.tile([P, CAPS, CAP_DIM], F32, name="centred", bufs=2)
@@ -278,7 +273,7 @@ def tile_hotpatchcapsmodel_pa_kernel(
             for c in range(HALVES):
                 nc.tensor.matmul(
                     out=flat[:, P * c : P * (c + 1)],
-                    lhsT=s["biased_t"][:, c, :],
+                    lhsT=s["biased_t"][c][:],
                     rhs=centre[:],
                     start=True,
                     stop=True,
@@ -336,7 +331,6 @@ def tile_hotpatchcapsmodel_pa_kernel(
             (capsule_sums, 8),
             (squares, 3),
             (quantise_h1, 1),
-            (mean, 3),
             (interleave_h, 6),
             (capsule_rstd, 8),
             (transpose_h1, 0),
@@ -351,11 +345,11 @@ def tile_hotpatchcapsmodel_pa_kernel(
                     spread_b2()
                     order_w2_codes()
                     interleave_pc_w()
-                if step == 2:
-                    order_w2_plane()
                 if step == 4:
                     quantise_pc_w()
                 for stage, behind in STEP:
                     t = step - behind
                     if 0 <= t < TILES:
                         stage(t, state[t])
+                    if stage == interleave_h1 and t == 0:
+                        order_w2_plane()

@@ -60,6 +60,7 @@ def tile_hotpatchcapsmodel_pa_kernel(
             )
         nc.sync.dma_start(out=b2_rows[0:1, :], in_=b2.unsqueeze(0))
         nc.sync.dma_start(out=h1_sb[:, 1:4, :], in_=h1_rows[:, 1:4, :])
+        nc.sync.dma_start(out=h1_sb[:, 4:8, :], in_=h1_rows[:, 4:8, :])
         pw_raw = keep.tile([P, CAPS, PACK * CAP_DIM], BF16)
         nc.sync.dma_start(out=pw_raw[:], in_=pc_W.rearrange("n (p j) q -> p n (j q)", j=PACK))
         ln_g_raw = keep.tile([P, PACK], BF16)
@@ -70,7 +71,6 @@ def tile_hotpatchcapsmodel_pa_kernel(
         for c in range(HALVES):
             rows = slice(CAPS // HALVES * c, CAPS // HALVES * (c + 1))
             nc.sync.dma_start(out=pc_b_col[c][:], in_=pc_b[rows, :].rearrange("n q -> (n q)").unsqueeze(1))
-        nc.sync.dma_start(out=h1_sb[:, 4:8, :], in_=h1_rows[:, 4:8, :])
         nc.sync.dma_start(out=h1_sb[:, 8:16, :], in_=h1_rows[:, 8:16, :])
         pcg_bc = keep.tile([P, NP], BF16)
         nc.sync.dma_start(out=pcg_bc[:], in_=pc_g.rearrange("n q -> (n q)").partition_broadcast(P))
@@ -345,7 +345,7 @@ def tile_hotpatchcapsmodel_pa_kernel(
                     spread_b2()
                     order_w2_codes()
                     interleave_pc_w()
-                if step == 4:
+                if step == 7:
                     quantise_pc_w()
                 for stage, behind in STEP:
                     t = step - behind

@@ -22,6 +22,8 @@ HALVES = NP // P
 TILES = B // P
 EPS = 1e-5
 
+UNORDERED = 3
+
 FLOPS = 2 * B * H1 * E + 2 * B * E * NP
 
 
@@ -47,7 +49,8 @@ def tile_hotpatchcapsmodel_pa_kernel(
         nc.vector.memset(ones[:], 1.0)
 
         h1_sb = keep.tile([P, TILES, H1], BF16)
-        nc.sync.dma_start(out=h1_sb[:, 0:1, :], in_=h1_rows[:, 0:1, :])
+        nc.sync.dma_start(out=h1_sb[:, 0:2, :], in_=h1_rows[:, 0:2, :])
+        nc.sync.dma_start(out=b2_rows[0:1, :], in_=b2.unsqueeze(0))
         w2_codes_raw = keep.tile([P, E], U32, align_bytes=64)
         nc.sync.dma_start(
             out=w2_codes_raw[:].bitcast(I32),
@@ -58,8 +61,7 @@ def tile_hotpatchcapsmodel_pa_kernel(
                 out=w2_plane_raw[32 * quadrant : 32 * quadrant + 4, :].bitcast(I32),
                 in_=W2_scales[0, 4 * quadrant : 4 * quadrant + 4, :].bitcast(I32),
             )
-        nc.sync.dma_start(out=b2_rows[0:1, :], in_=b2.unsqueeze(0))
-        nc.sync.dma_start(out=h1_sb[:, 1:4, :], in_=h1_rows[:, 1:4, :])
+        nc.sync.dma_start(out=h1_sb[:, 2:4, :], in_=h1_rows[:, 2:4, :])
         nc.sync.dma_start(out=h1_sb[:, 4:8, :], in_=h1_rows[:, 4:8, :])
         pw_raw = keep.tile([P, CAPS, PACK * CAP_DIM], BF16)
         nc.sync.dma_start(out=pw_raw[:], in_=pc_W.rearrange("n (p j) q -> p n (j q)", j=PACK))
@@ -100,7 +102,9 @@ def tile_hotpatchcapsmodel_pa_kernel(
         w2_codes = keep.tile([P, E], U32, align_bytes=64)
         w2_plane = keep.tile([P, E], U8, align_bytes=64)
         b2_bc = keep.tile([P, E], F32)
+        b2_bc_raw = keep.tile([P, E], F32)
         ln_g_col = keep.tile([P, PACK], F32)
+        ln_b_col32 = keep.tile([P, PACK], F32)
         pw_grouped = keep.tile([P, CAPS, CAP_DIM, PACK], BF16, align_bytes=64)
         pw_codes = keep.tile([P, NP], U32, align_bytes=64)
         pw_plane = keep.tile([P, NP], U8, align_bytes=64)
@@ -118,8 +122,9 @@ def tile_hotpatchcapsmodel_pa_kernel(
             )
 
         def spread_b2():
-            b2_spread = psum.tile([P, E], F32, name="b2_spread", tag="acc")
+            b2_spread = psum.tile([P, E], F32, name="b2_spread", tag="centred", bufs=2)
             nc.tensor.matmul(out=b2_spread[:], lhsT=ones[:], rhs=b2_rows[:], start=True, stop=True)
+            nc.scalar.copy(out=b2_bc_raw[:], in_=b2_spread[:])
             nc.scalar.copy(
                 out=b2_bc[:].rearrange("r (j p) -> r j p", j=PACK),
                 in_=b2_spread[:].rearrange("r (p j) -> r j p", j=PACK),
@@ -127,6 +132,7 @@ def tile_hotpatchcapsmodel_pa_kernel(
 
         def interleave_pc_w():
             nc.gpsimd.tensor_copy(out=ln_g_col[:], in_=ln_g_raw[:])
+            nc.gpsimd.tensor_copy(out=ln_b_col32[:], in_=ln_b_col[:])
             nc.gpsimd.tensor_scalar(
                 out=pw_grouped[:],
                 in0=pw_raw[:].rearrange("p n (j q) -> p n q j", j=PACK),
@@ -166,15 +172,16 @@ def tile_hotpatchcapsmodel_pa_kernel(
                 out=s["acc"][:],
                 lhsT=s["h1_codes"][:].bitcast(FP8X4),
                 lhsT_scale=s["h1_plane"][:],
-                rhs=w2_codes[:].bitcast(FP8X4),
-                rhs_scale=w2_plane[:],
+                rhs=(w2_codes_raw if t < UNORDERED else w2_codes)[:].bitcast(FP8X4),
+                rhs_scale=(w2_plane_raw if t < UNORDERED else w2_plane)[:],
                 start=True,
                 stop=True,
             )
 
         def add_b2(t, s):
             s["z"] = work.tile([P, E], F32, name="z")
-            nc.vector.tensor_tensor(out=s["z"][:], in0=s["acc"][:], in1=b2_bc[:], op=ALU.add)
+            b2_columns = b2_bc_raw if t < UNORDERED else b2_bc
+            nc.vector.tensor_tensor(out=s["z"][:], in0=s["acc"][:], in1=b2_columns[:], op=ALU.add)
 
         def relu(t, s):
             s["z_sum"] = work.tile([P, 1], F32, name="z_sum")
@@ -202,9 +209,13 @@ def tile_hotpatchcapsmodel_pa_kernel(
 
         def normalise(t, s):
             s["normed"] = work.tile([P, E], F32, name="normed")
+            normed, z = s["normed"][:], s["z"][:]
+            if t < UNORDERED:
+                normed = normed.rearrange("r (j p) -> r p j", j=PACK)
+                z = z.rearrange("r (p j) -> r p j", j=PACK)
             nc.vector.tensor_scalar(
-                out=s["normed"][:],
-                in0=s["z"][:],
+                out=normed,
+                in0=z,
                 scalar1=s["neg_mean"][:],
                 scalar2=s["rstd"][:],
                 op0=ALU.add,
@@ -212,20 +223,33 @@ def tile_hotpatchcapsmodel_pa_kernel(
             )
 
         def transpose_h(t, s):
-            s["normed_t"] = psum.tile([P, PACK, P], F32, name="normed_t", bufs=2)
+            normed_t = psum.tile([P, PACK - 1, P], F32, name="normed_t", bufs=2)
+            last_t = psum.tile([P, P], F32, name="last_t")
+            s["normed_t"] = [normed_t[:, j, :] for j in range(PACK - 1)] + [last_t[:]]
             for j in range(PACK):
-                nc.tensor.transpose(s["normed_t"][:, j, :], s["normed"][:, P * j : P * (j + 1)], ident[:])
+                nc.tensor.transpose(s["normed_t"][j], s["normed"][:, P * j : P * (j + 1)], ident[:])
 
         def affine(t, s):
-            s["h_t"] = work.tile([P, PACK, P], BF16, name="h_t")
-            for j in range(PACK):
+            for j in range(PACK - 1):
                 nc.scalar.activation(
                     out=s["h_t"][:, j, :],
-                    in_=s["normed_t"][:, j, :],
+                    in_=s["normed_t"][j],
                     func=ACT.Identity,
                     bias=ln_b_col[:, j : j + 1],
                     scale=ln_g_col[:, j : j + 1],
                 )
+
+        def affine_last(t, s):
+            j = PACK - 1
+            s["h_t"] = work.tile([P, PACK, P], BF16, name="h_t")
+            nc.vector.tensor_scalar(
+                out=s["h_t"][:, j, :],
+                in0=s["normed_t"][j],
+                scalar1=ln_g_col[:, j : j + 1],
+                scalar2=ln_b_col32[:, j : j + 1],
+                op0=ALU.mult,
+                op1=ALU.add,
+            )
 
         def interleave_h(t, s):
             s["h_grouped"] = work.tile([P, P, PACK], BF16, name="h_grouped", align_bytes=64)
@@ -244,12 +268,11 @@ def tile_hotpatchcapsmodel_pa_kernel(
             )
 
         def second_product(t, s):
-            s["prim_t"] = []
+            s["prim_t"] = psum.tile([P, HALVES, P], F32, name="prim_t")
             for c in range(HALVES):
-                s["prim_t"].append(psum.tile([P, P], F32, name="prim_t", bufs=HALVES))
                 cols = slice(P * c, P * (c + 1))
                 nc.tensor.matmul_mx(
-                    out=s["prim_t"][c][:],
+                    out=s["prim_t"][:, c, :],
                     lhsT=pw_codes[:, cols].bitcast(FP8X4),
                     lhsT_scale=pw_plane[:, cols],
                     rhs=s["h_codes"][:].bitcast(FP8X4),
@@ -260,12 +283,10 @@ def tile_hotpatchcapsmodel_pa_kernel(
 
         def add_pc_b(t, s):
             s["biased_t"] = [work.tile([P, P], F32, name="biased_t%d" % c) for c in range(HALVES)]
-            nc.scalar.activation(
-                out=s["biased_t"][0][:], in_=s["prim_t"][0][:], func=ACT.Identity, bias=pc_b_col[0][:], scale=1.0
-            )
-            nc.vector.tensor_scalar(
-                out=s["biased_t"][1][:], in0=s["prim_t"][1][:], scalar1=pc_b_col[1][:], scalar2=None, op0=ALU.add
-            )
+            for c in range(HALVES):
+                nc.scalar.activation(
+                    out=s["biased_t"][c][:], in_=s["prim_t"][:, c, :], func=ACT.Identity, bias=pc_b_col[c][:], scale=1.0
+                )
 
         def take_means_off(t, s):
             s["centred"] = psum.tile([P, CAPS, CAP_DIM], F32, name="centred", bufs=2)
@@ -297,18 +318,30 @@ def tile_hotpatchcapsmodel_pa_kernel(
                 scale=1.0 / CAP_DIM,
             )
 
+        def gain_last(t, s):
+            if t == TILES - 1:
+                s["gained"] = work.tile([P, CAPS, CAP_DIM], F32, name="gained")
+                nc.vector.tensor_tensor(
+                    out=s["gained"][:],
+                    in0=s["centred"][:],
+                    in1=pcg_bc[:].rearrange("p (m q) -> p m q", q=CAP_DIM),
+                    op=ALU.mult,
+                )
+
         def scale_capsules(t, s):
             s["result"] = work.tile([P, NP], F32, name="result")
             nc.vector.tensor_tensor(
                 out=s["result"][:].rearrange("p (m q) -> p m q", q=CAP_DIM),
-                in0=s["centred"][:],
+                in0=(s["gained"] if t == TILES - 1 else s["centred"])[:],
                 in1=s["cap_rstd"][:].unsqueeze(2).to_broadcast([P, CAPS, CAP_DIM]),
                 op=ALU.mult,
             )
 
         def gain_and_shift(t, s):
-            engine = nc.vector if t == TILES - 1 else nc.gpsimd
-            engine.tensor_tensor(out=s["result"][:], in0=s["result"][:], in1=pcg_bc[:], op=ALU.mult)
+            engine = nc.vector
+            if t < TILES - 1:
+                engine = nc.gpsimd
+                engine.tensor_tensor(out=s["result"][:], in0=s["result"][:], in1=pcg_bc[:], op=ALU.mult)
             engine.tensor_tensor(out=s["result"][:], in0=s["result"][:], in1=pcbeta_bc[:], op=ALU.add)
 
         def store(t, s):
@@ -319,6 +352,7 @@ def tile_hotpatchcapsmodel_pa_kernel(
             (gain_and_shift, 9),
             (store, 9),
             (interleave_h1, 1),
+            (affine_last, 6),
             (rstd, 4),
             (take_means_off, 8),
             (first_product, 2),
@@ -329,6 +363,7 @@ def tile_hotpatchcapsmodel_pa_kernel(
             (add_b2, 2),
             (add_pc_b, 7),
             (capsule_sums, 8),
+            (gain_last, 8),
             (squares, 3),
             (quantise_h1, 1),
             (interleave_h, 6),
@@ -343,7 +378,6 @@ def tile_hotpatchcapsmodel_pa_kernel(
             for step in range(TILES + 9):
                 if step == 1:
                     spread_b2()
-                    order_w2_codes()
                     interleave_pc_w()
                 if step == 7:
                     quantise_pc_w()
@@ -351,5 +385,7 @@ def tile_hotpatchcapsmodel_pa_kernel(
                     t = step - behind
                     if 0 <= t < TILES:
                         stage(t, state[t])
-                    if stage == interleave_h1 and t == 0:
+                    if stage == quantise_h1 and t == 1:
+                        order_w2_codes()
+                    if stage == quantise_h1 and t == 2:
                         order_w2_plane()

@@ -33,7 +33,7 @@ def tile_hotpatchcapsmodel_pa_kernel(
     nc = tc.nc
     with ExitStack() as ctx:
         keep = ctx.enter_context(tc.tile_pool(name="keep", bufs=1))
-        work = ctx.enter_context(tc.tile_pool(name="work", bufs=4))
+        work = ctx.enter_context(tc.tile_pool(name="work", bufs=8))
         psum = ctx.enter_context(tc.psum_pool(name="psum", bufs=1))
 
         h1_rows = h1.rearrange("(p t) k -> p t k", t=TILES)

from contextlib import ExitStack

import concourse.mybir as mybir
from concourse.masks import make_identity

F32 = mybir.dt.float32
BF16 = mybir.dt.bfloat16
I32 = mybir.dt.int32
U32 = mybir.dt.uint32
U8 = mybir.dt.uint8
FP8X4 = mybir.dt.float8_e4m3fn_x4
ALU = mybir.AluOpType
ACT = mybir.ActivationFunctionType
AXIS = mybir.AxisListType

P = 128
PACK = 4
B, H1, E = 2048, 512, 512
CAPS, CAP_DIM = 32, 8
NP = CAPS * CAP_DIM
HALVES = NP // P
TILES = B // P
EPS = 1e-5

UNORDERED = 3

FLOPS = 2 * B * H1 * E + 2 * B * E * NP


def tile_hotpatchcapsmodel_pa_kernel(
    tc, h1, W2_words, W2_scales, b2, ln_g, ln_b, pc_W, pc_b, pc_g, pc_beta, out
):
    nc = tc.nc
    with ExitStack() as ctx:
        keep = ctx.enter_context(tc.tile_pool(name="keep", bufs=1))
        work = ctx.enter_context(tc.tile_pool(name="work", bufs=8))
        psum = ctx.enter_context(tc.psum_pool(name="psum", bufs=1))

        h1_rows = h1.rearrange("(p t) k -> p t k", t=TILES)
        out_rows = out.rearrange("(p t) n q -> p t (n q)", t=TILES)

        w2_plane_raw = keep.tile([P, E], U8, align_bytes=64)
        nc.vector.memset(w2_plane_raw[:].bitcast(I32), 0)
        b2_rows = keep.tile([P, E], BF16)
        nc.gpsimd.memset(b2_rows[:], 0.0)
        eps = keep.tile([P, 1], F32)
        nc.vector.memset(eps[:], EPS)
        ones = keep.tile([P, P], BF16)
        nc.vector.memset(ones[:], 1.0)

        h1_sb = keep.tile([P, TILES, H1], BF16)
        nc.sync.dma_start(out=h1_sb[:, 0:2, :], in_=h1_rows[:, 0:2, :])
        nc.sync.dma_start(out=b2_rows[0:1, :], in_=b2.unsqueeze(0))
        w2_codes_raw = keep.tile([P, E], U32, align_bytes=64)
        nc.sync.dma_start(
            out=w2_codes_raw[:].bitcast(I32),
            in_=W2_words[0].rearrange("p n t -> p (n t)").bitcast(I32),
        )
        for quadrant in range(4):
            nc.sync.dma_start(
                out=w2_plane_raw[32 * quadrant : 32 * quadrant + 4, :].bitcast(I32),
                in_=W2_scales[0, 4 * quadrant : 4 * quadrant + 4, :].bitcast(I32),
            )
        nc.sync.dma_start(out=h1_sb[:, 2:4, :], in_=h1_rows[:, 2:4, :])
        nc.sync.dma_start(out=h1_sb[:, 4:8, :], in_=h1_rows[:, 4:8, :])
        pw_raw = keep.tile([P, CAPS, PACK * CAP_DIM], BF16)
        nc.sync.dma_start(out=pw_raw[:], in_=pc_W.rearrange("n (p j) q -> p n (j q)", j=PACK))
        ln_g_raw = keep.tile([P, PACK], BF16)
        nc.sync.dma_start(out=ln_g_raw[:], in_=ln_g.rearrange("(p j) -> p j", j=PACK))
        ln_b_col = keep.tile([P, PACK], BF16)
        nc.sync.dma_start(out=ln_b_col[:], in_=ln_b.rearrange("(p j) -> p j", j=PACK))
        pc_b_col = [keep.tile([P, 1], BF16, name="pc_b_col%d" % c) for c in range(HALVES)]
        for c in range(HALVES):
            rows = slice(CAPS // HALVES * c, CAPS // HALVES * (c + 1))
            nc.sync.dma_start(out=pc_b_col[c][:], in_=pc_b[rows, :].rearrange("n q -> (n q)").unsqueeze(1))
        nc.sync.dma_start(out=h1_sb[:, 8:16, :], in_=h1_rows[:, 8:16, :])
        pcg_bc = keep.tile([P, NP], BF16)
        nc.sync.dma_start(out=pcg_bc[:], in_=pc_g.rearrange("n q -> (n q)").partition_broadcast(P))
        pcbeta_bc = keep.tile([P, NP], BF16)
        nc.sync.dma_start(out=pcbeta_bc[:], in_=pc_beta.rearrange("n q -> (n q)").partition_broadcast(P))

        warm = keep.tile([P, 1], F32)
        nc.scalar.activation(out=warm[:], in_=eps[:], func=ACT.Abs_reciprocal_sqrt)

        ident = keep.tile([P, P], F32)
        make_identity(nc, ident[:])

        same_capsule = keep.tile([P, P // CAP_DIM], F32)
        nc.vector.tensor_reduce(
            out=same_capsule[:], in_=ident[:].rearrange("p (n q) -> p n q", q=CAP_DIM), axis=AXIS.X, op=ALU.add
        )
        centre = keep.tile([P, P], F32)
        nc.vector.scalar_tensor_tensor(
            out=centre[:].rearrange("p (n q) -> p n q", q=CAP_DIM),
            in0=same_capsule[:].unsqueeze(2).to_broadcast([P, P // CAP_DIM, CAP_DIM]),
            scalar=-1.0 / CAP_DIM,
            in1=ident[:].rearrange("p (n q) -> p n q", q=CAP_DIM),
            op0=ALU.mult,
            op1=ALU.add,
        )

        w2_codes = keep.tile([P, E], U32, align_bytes=64)
        w2_plane = keep.tile([P, E], U8, align_bytes=64)
        b2_bc = keep.tile([P, E], F32)
        b2_bc_raw = keep.tile([P, E], F32)
        ln_g_col = keep.tile([P, PACK], F32)
        ln_b_col32 = keep.tile([P, PACK], F32)
        pw_grouped = keep.tile([P, CAPS, CAP_DIM, PACK], BF16, align_bytes=64)
        pw_codes = keep.tile([P, NP], U32, align_bytes=64)
        pw_plane = keep.tile([P, NP], U8, align_bytes=64)

        def order_w2_codes():
            nc.vector.tensor_copy(
                out=w2_codes[:].bitcast(I32).rearrange("k (j p) -> k p j", j=PACK),
                in_=w2_codes_raw[:].bitcast(I32).rearrange("k (p j) -> k p j", j=PACK),
            )

        def order_w2_plane():
            nc.vector.tensor_copy(
                out=w2_plane[:].rearrange("k (j p) -> k p j", j=PACK),
                in_=w2_plane_raw[:].rearrange("k (p j) -> k p j", j=PACK),
            )

        def spread_b2():
            b2_spread = psum.tile([P, E], F32, name="b2_spread", tag="centred", bufs=2)
            nc.tensor.matmul(out=b2_spread[:], lhsT=ones[:], rhs=b2_rows[:], start=True, stop=True)
            nc.scalar.copy(out=b2_bc_raw[:], in_=b2_spread[:])
            nc.scalar.copy(
                out=b2_bc[:].rearrange("r (j p) -> r j p", j=PACK),
                in_=b2_spread[:].rearrange("r (p j) -> r j p", j=PACK),
            )

        def interleave_pc_w():
            nc.gpsimd.tensor_copy(out=ln_g_col[:], in_=ln_g_raw[:])
            nc.gpsimd.tensor_copy(out=ln_b_col32[:], in_=ln_b_col[:])
            nc.gpsimd.tensor_scalar(
                out=pw_grouped[:],
                in0=pw_raw[:].rearrange("p n (j q) -> p n q j", j=PACK),
                scalar1=1.0,
                scalar2=0.0,
                op0=ALU.mult,
                op1=ALU.add,
            )

        def quantise_pc_w():
            nc.vector.quantize_mx(
                out=pw_codes[:].bitcast(FP8X4), scales=pw_plane[:], in_=pw_grouped[:].rearrange("p n q j -> p (n q j)")
            )

        def transpose_h1(t, s):
            s["h1_t"] = psum.tile([P, 2, P], F32, name="h1_t")
            words = h1_sb[:, t, :].bitcast(F32)
            for u in range(2):
                nc.tensor.transpose(s["h1_t"][:, u, :], words[:, u : H1 // 2 : 2], ident[:])

        def interleave_h1(t, s):
            s["h1_grouped"] = work.tile([P, P, PACK], BF16, name="h1_grouped", align_bytes=64)
            nc.vector.tensor_copy(out=s["h1_grouped"][:].bitcast(F32), in_=s["h1_t"][:].rearrange("p u r -> p r u"))

        def quantise_h1(t, s):
            s["h1_codes"] = work.tile([P, P], U32, name="h1_codes", align_bytes=64)
            s["h1_plane"] = work.tile([P, P], U8, name="h1_plane", align_bytes=64)
            nc.vector.quantize_mx(
                out=s["h1_codes"][:].bitcast(FP8X4),
                scales=s["h1_plane"][:],
                in_=s["h1_grouped"][:].rearrange("p r k -> p (r k)"),
            )

        def first_product(t, s):
            s["acc"] = psum.tile([P, E], F32, name="acc", tag="acc")
            nc.tensor.matmul_mx(
                out=s["acc"][:],
                lhsT=s["h1_codes"][:].bitcast(FP8X4),
                lhsT_scale=s["h1_plane"][:],
                rhs=(w2_codes_raw if t < UNORDERED else w2_codes)[:].bitcast(FP8X4),
                rhs_scale=(w2_plane_raw if t < UNORDERED else w2_plane)[:],
                start=True,
                stop=True,
            )

        def add_b2(t, s):
            s["z"] = work.tile([P, E], F32, name="z")
            b2_columns = b2_bc_raw if t < UNORDERED else b2_bc
            nc.vector.tensor_tensor(out=s["z"][:], in0=s["acc"][:], in1=b2_columns[:], op=ALU.add)

        def relu(t, s):
            s["z_sum"] = work.tile([P, 1], F32, name="z_sum")
            nc.scalar.activation(out=s["z"][:], in_=s["z"][:], func=ACT.Relu, accum_out=s["z_sum"][:])

        def squares(t, s):
            s["sq_sum"] = work.tile([P, 1], F32, name="sq_sum")
            unused = work.tile([P, E], BF16, name="unused")
            nc.scalar.activation(
                out=unused[:],
                in_=s["z"][:],
                func=ACT.Square,
                bias=s["z_sum"][:],
                scale=-float(E),
                accum_out=s["sq_sum"][:],
            )

        def rstd(t, s):
            s["neg_mean"] = work.tile([P, 1], F32, name="neg_mean")
            nc.scalar.mul(out=s["neg_mean"][:], in_=s["z_sum"][:], mul=-1.0 / E)
            s["rstd"] = work.tile([P, 1], F32, name="rstd")
            nc.scalar.activation(
                out=s["rstd"][:], in_=s["sq_sum"][:], func=ACT.Abs_reciprocal_sqrt, bias=eps[:], scale=1.0 / float(E) ** 3
            )

        def normalise(t, s):
            s["normed"] = work.tile([P, E], F32, name="normed")
            normed, z = s["normed"][:], s["z"][:]
            if t < UNORDERED:
                normed = normed.rearrange("r (j p) -> r p j", j=PACK)
                z = z.rearrange("r (p j) -> r p j", j=PACK)
            nc.vector.tensor_scalar(
                out=normed,
                in0=z,
                scalar1=s["neg_mean"][:],
                scalar2=s["rstd"][:],
                op0=ALU.add,
                op1=ALU.mult,
            )

        def transpose_h(t, s):
            normed_t = psum.tile([P, PACK - 1, P], F32, name="normed_t", bufs=2)
            last_t = psum.tile([P, P], F32, name="last_t")
            s["normed_t"] = [normed_t[:, j, :] for j in range(PACK - 1)] + [last_t[:]]
            for j in range(PACK):
                nc.tensor.transpose(s["normed_t"][j], s["normed"][:, P * j : P * (j + 1)], ident[:])

        def affine(t, s):
            for j in range(PACK - 1):
                nc.scalar.activation(
                    out=s["h_t"][:, j, :],
                    in_=s["normed_t"][j],
                    func=ACT.Identity,
                    bias=ln_b_col[:, j : j + 1],
                    scale=ln_g_col[:, j : j + 1],
                )

        def affine_last(t, s):
            j = PACK - 1
            s["h_t"] = work.tile([P, PACK, P], BF16, name="h_t")
            nc.vector.tensor_scalar(
                out=s["h_t"][:, j, :],
                in0=s["normed_t"][j],
                scalar1=ln_g_col[:, j : j + 1],
                scalar2=ln_b_col32[:, j : j + 1],
                op0=ALU.mult,
                op1=ALU.add,
            )

        def interleave_h(t, s):
            s["h_grouped"] = work.tile([P, P, PACK], BF16, name="h_grouped", align_bytes=64)
            nc.vector.tensor_copy(
                out=s["h_grouped"][:].rearrange("p (c x) j -> p c j x", x=4),
                in_=s["h_t"][:].rearrange("p j (c x) -> p c j x", x=4),
            )

        def quantise_h(t, s):
            s["h_codes"] = work.tile([P, P], U32, name="h_codes", align_bytes=64)
            s["h_plane"] = work.tile([P, P], U8, name="h_plane", align_bytes=64)
            nc.vector.quantize_mx(
                out=s["h_codes"][:].bitcast(FP8X4),
                scales=s["h_plane"][:],
                in_=s["h_grouped"][:].rearrange("p r j -> p (r j)"),
            )

        def second_product(t, s):
            s["prim_t"] = psum.tile([P, HALVES, P], F32, name="prim_t")
            for c in range(HALVES):
                cols = slice(P * c, P * (c + 1))
                nc.tensor.matmul_mx(
                    out=s["prim_t"][:, c, :],
                    lhsT=pw_codes[:, cols].bitcast(FP8X4),
                    lhsT_scale=pw_plane[:, cols],
                    rhs=s["h_codes"][:].bitcast(FP8X4),
                    rhs_scale=s["h_plane"][:],
                    start=True,
                    stop=True,
                )

        def add_pc_b(t, s):
            s["biased_t"] = [work.tile([P, P], F32, name="biased_t%d" % c) for c in range(HALVES)]
            for c in range(HALVES):
                nc.scalar.activation(
                    out=s["biased_t"][c][:], in_=s["prim_t"][:, c, :], func=ACT.Identity, bias=pc_b_col[c][:], scale=1.0
                )

        def take_means_off(t, s):
            s["centred"] = psum.tile([P, CAPS, CAP_DIM], F32, name="centred", bufs=2)
            flat = s["centred"][:].rearrange("p m q -> p (m q)")
            for c in range(HALVES):
                nc.tensor.matmul(
                    out=flat[:, P * c : P * (c + 1)],
                    lhsT=s["biased_t"][c][:],
                    rhs=centre[:],
                    start=True,
                    stop=True,
                )

        def capsule_squares(t, s):
            s["cap_squares"] = work.tile([P, CAPS, CAP_DIM], F32, name="cap_squares")
            nc.scalar.activation(out=s["cap_squares"][:], in_=s["centred"][:], func=ACT.Square)

        def capsule_sums(t, s):
            s["cap_sq_sum"] = work.tile([P, CAPS], F32, name="cap_sq_sum")
            nc.vector.tensor_reduce(out=s["cap_sq_sum"][:], in_=s["cap_squares"][:], axis=AXIS.X, op=ALU.add)

        def capsule_rstd(t, s):
            s["cap_rstd"] = work.tile([P, CAPS], F32, name="cap_rstd")
            nc.scalar.activation(
                out=s["cap_rstd"][:],
                in_=s["cap_sq_sum"][:],
                func=ACT.Abs_reciprocal_sqrt,
                bias=eps[:],
                scale=1.0 / CAP_DIM,
            )

        def gain_last(t, s):
            if t == TILES - 1:
                s["gained"] = work.tile([P, CAPS, CAP_DIM], F32, name="gained")
                nc.vector.tensor_tensor(
                    out=s["gained"][:],
                    in0=s["centred"][:],
                    in1=pcg_bc[:].rearrange("p (m q) -> p m q", q=CAP_DIM),
                    op=ALU.mult,
                )

        def scale_capsules(t, s):
            s["result"] = work.tile([P, NP], F32, name="result")
            nc.vector.tensor_tensor(
                out=s["result"][:].rearrange("p (m q) -> p m q", q=CAP_DIM),
                in0=(s["gained"] if t == TILES - 1 else s["centred"])[:],
                in1=s["cap_rstd"][:].unsqueeze(2).to_broadcast([P, CAPS, CAP_DIM]),
                op=ALU.mult,
            )

        def gain_and_shift(t, s):
            engine = nc.vector
            if t < TILES - 1:
                engine = nc.gpsimd
                engine.tensor_tensor(out=s["result"][:], in0=s["result"][:], in1=pcg_bc[:], op=ALU.mult)
            engine.tensor_tensor(out=s["result"][:], in0=s["result"][:], in1=pcbeta_bc[:], op=ALU.add)

        def store(t, s):
            nc.sync.dma_start(out=out_rows[:, t, :], in_=s["result"][:])

        STEP = [
            (scale_capsules, 9),
            (gain_and_shift, 9),
            (store, 9),
            (interleave_h1, 1),
            (affine_last, 6),
            (rstd, 4),
            (take_means_off, 8),
            (first_product, 2),
            (second_product, 7),
            (affine, 6),
            (capsule_squares, 8),
            (transpose_h, 5),
            (add_b2, 2),
            (add_pc_b, 7),
            (capsule_sums, 8),
            (gain_last, 8),
            (squares, 3),
            (quantise_h1, 1),
            (interleave_h, 6),
            (capsule_rstd, 8),
            (transpose_h1, 0),
            (normalise, 4),
            (quantise_h, 6),
            (relu, 2),
        ]
        state = [{} for t in range(TILES)]
        with tc.manual_schedule():
            for step in range(TILES + 9):
                if step == 1:
                    spread_b2()
                    interleave_pc_w()
                if step == 7:
                    quantise_pc_w()
                for stage, behind in STEP:
                    t = step - behind
                    if 0 <= t < TILES:
                        stage(t, state[t])
                    if stage == quantise_h1 and t == 1:
                        order_w2_codes()
                    if stage == quantise_h1 and t == 2:
                        order_w2_plane()
